import numpy as np
import ml_dtypes


def mxq(x, axis, fmt="e4m3"):
    dtype, down = {"e4m3": (ml_dtypes.float8_e4m3fn, 7), "e5m2": (ml_dtypes.float8_e5m2, 14)}[fmt]
    v = np.moveaxis(np.asarray(x, np.float32).astype(ml_dtypes.bfloat16).astype(np.float64), axis, -1)
    blocks = v.reshape(v.shape[:-1] + (-1, 32))
    amax = np.abs(blocks).max(-1, keepdims=True)
    byte = np.maximum(np.where(amax > 0, np.frexp(amax)[1] - 1 + 127, 0) - down, 1)
    scale = np.exp2(byte - 127.0)
    codes = (blocks / scale).astype(np.float32).astype(dtype).astype(np.float64)
    return np.moveaxis((codes * scale).reshape(v.shape), -1, axis)


WIDE = False


def mx_kscale(k):
    if not WIDE:
        return np.ones(k)
    levels = np.array([10, -10, 5, -5, 0])
    a = np.random.permutation(np.resize(levels, k // 512 * 4)).reshape(k // 512, 4)
    idx = np.arange(k)
    return np.exp2(a[idx // 512, idx % 128 // 32])


BF16 = ml_dtypes.bfloat16


def bf(x):
    return np.asarray(x, np.float32).astype(BF16)


def f64(x):
    return np.asarray(x).astype(np.float64)


B, N, H, F, M, G, C = 16, 32, 512, 1024, 128, 1024, 3


def silu(v):
    return v / (1.0 + np.exp(-v))


def setup_inputs():
    s = mx_kscale(H)
    w_nodes = np.random.standard_normal((2, H, F)) / np.sqrt(2 * H) / s[None, :, None]
    w_dist = np.random.standard_normal((1, F)) * 0.3
    return {"node_state": bf(np.random.standard_normal((B, N, H)) * s),
            "positions": bf(np.random.standard_normal((B, N, C))),
            "We1": bf(np.concatenate([w_nodes.reshape(2 * H, F), w_dist], 0)),
            "be1": bf(np.random.standard_normal(F) * 0.5),
            "We2": bf(np.random.standard_normal((F, M)) / np.sqrt(F)),
            "be2": bf(np.random.standard_normal(M) * 0.5)}


def reference(node_state, positions, We1, be1, We2, be2):
    x, p, w1 = f64(node_state), f64(positions), f64(We1)
    rel = p[:, :, None, :] - p[:, None, :, :]
    sq = np.sum(rel * rel, axis=-1, keepdims=True)
    dist = np.where(sq > 0, np.sqrt(np.where(sq > 0, sq, 1.0)), 0.0)
    xq = mxq(x, 2, "e4m3")
    a_i = xq @ mxq(w1[:H], 0, "e4m3")
    a_j = xq @ mxq(w1[H:2 * H], 0, "e4m3")
    pre = a_i[:, :, None, :] + a_j[:, None, :, :] + dist * w1[2 * H] + f64(be1)
    h = silu(pre).reshape(B * N * N, F)
    msg = (mxq(h, 1, "e4m3") @ mxq(f64(We2), 0, "e4m3")) + f64(be2)
    return msg.reshape(B, N, N, M)

@@ -1,0 +1,283 @@
+from contextlib import ExitStack
+
+import concourse.mybir as mybir
+from concourse.masks import make_identity
+
+F32 = mybir.dt.float32
+BF16 = mybir.dt.bfloat16
+U32 = mybir.dt.uint32
+U8 = mybir.dt.uint8
+FP8X4 = mybir.dt.float8_e4m3fn_x4
+ALU = mybir.AluOpType
+ACT = mybir.ActivationFunctionType
+AXIS = mybir.AxisListType
+
+P = 128
+PACK = 4
+K_PASS = P * PACK
+
+GRAPHS = 16
+NODES = 32
+COORDS = 3
+H = 512
+F = 1024
+M = 128
+
+COLS = NODES * GRAPHS
+F_BLOCKS = F // P
+F_PASSES = F // K_PASS
+ROW_BLOCKS = COLS // P
+BLOCK_NODES = P // GRAPHS
+SHIFTS = NODES // 2 + 1
+
+COPIES = 4
+WINDOW_STEP = COPIES * GRAPHS
+COPY_COLS = 2 * COLS
+STATE_COLS = COPY_COLS + (COPIES - 1) * GRAPHS
+
+REACH = (ROW_BLOCKS - 1) * BLOCK_NODES + SHIFTS
+SMALLEST_SQUARE = 2.0**-100
+
+FLOPS = 2 * GRAPHS * NODES * H * 2 * F + 2 * GRAPHS * NODES * NODES * F * M
+
+
+def regroup(engine_copy, grouped, planes):
+    engine_copy(
+        out=grouped.rearrange("p (g i) t -> p g t i", i=4),
+        in_=planes.rearrange("p t (g i) -> p g t i", i=4),
+    )
+
+
+def tile_graphmessagelayer_pa_t_kernel(tc, node_state, positions, We1, be1, We2, be2, out):
+    nc = tc.nc
+    with ExitStack() as ctx:
+        keep = ctx.enter_context(tc.tile_pool(name="keep", bufs=1))
+        stage = ctx.enter_context(tc.tile_pool(name="stage", bufs=2))
+        work = ctx.enter_context(tc.tile_pool(name="work", bufs=3))
+        banks = ctx.enter_context(tc.psum_pool(name="banks", bufs=6))
+        msg_banks = ctx.enter_context(tc.psum_pool(name="msg_banks", bufs=2))
+
+        x_rows = keep.tile([P, GRAPHS // 4, H], BF16)
+        nc.sync.dma_start(out=x_rows[:], in_=node_state.rearrange("(g bl) u k -> (bl u) g k", bl=4))
+        w1_rows = keep.tile([P, 2 * PACK, F], BF16)
+        w1_view = We1[0 : 2 * H, :].rearrange("(j p) f -> p j f", p=P)
+        for c in range(F_PASSES):
+            f_half = slice(c * K_PASS, (c + 1) * K_PASS)
+            nc.sync.dma_start(out=w1_rows[:, :, f_half], in_=w1_view[:, :, f_half])
+        w2_rows = keep.tile([P, F_BLOCKS, M], BF16)
+        nc.sync.dma_start(out=w2_rows[:], in_=We2.rearrange("(j p) m -> p j m", p=P))
+
+        to_end = keep.tile([P, REACH, COORDS], BF16)
+        from_start = keep.tile([P, REACH, COORDS], BF16)
+        nc.vector.memset(to_end[:], 0.0)
+        nc.vector.memset(from_start[:], 0.0)
+        for lane in range(BLOCK_NODES):
+            rows = slice(lane * GRAPHS, (lane + 1) * GRAPHS)
+            left = NODES - lane
+            nc.scalar.dma_start(out=to_end[rows, 0:left, :], in_=positions[:, lane:NODES, :])
+            nc.scalar.dma_start(out=from_start[rows, left:REACH, :], in_=positions[:, 0 : REACH - left, :])
+        vectors = keep.tile([P, P], BF16)
+        nc.vector.memset(vectors[:], 0.0)
+        nc.scalar.dma_start(
+            out=vectors[0:F_BLOCKS, :], in_=We1[2 * H : 2 * H + 1, :].rearrange("o (j p) -> (o j) p", p=P)
+        )
+        nc.scalar.dma_start(out=vectors[F_BLOCKS : 2 * F_BLOCKS, :], in_=be1.rearrange("(j p) -> j p", p=P))
+        be2_rows = keep.tile([P, M], BF16)
+        nc.scalar.dma_start(out=be2_rows[:], in_=be2.partition_broadcast(P))
+
+        ident_bf16 = keep.tile([P, P], BF16)
+        make_identity(nc, ident_bf16[:])
+        ident_f32 = keep.tile([P, P], F32)
+        make_identity(nc, ident_f32[:])
+
+        around = keep.tile([P, REACH, COORDS], F32)
+        nc.vector.tensor_tensor(out=around[:], in0=to_end[:], in1=from_start[:], op=ALU.add)
+        delta = keep.tile([P, ROW_BLOCKS, SHIFTS, COORDS], F32)
+        for q in range(ROW_BLOCKS):
+            first = q * BLOCK_NODES
+            nc.vector.tensor_tensor(
+                out=delta[:, q],
+                in0=around[:, first : first + SHIFTS, :],
+                in1=around[:, first : first + 1, :].to_broadcast([P, SHIFTS, COORDS]),
+                op=ALU.subtract,
+            )
+        delta_sq = keep.tile([P, ROW_BLOCKS, SHIFTS, COORDS], F32)
+        nc.vector.tensor_tensor(out=delta_sq[:], in0=delta[:], in1=delta[:], op=ALU.mult)
+        square = keep.tile([P, ROW_BLOCKS, SHIFTS], F32)
+        nc.vector.tensor_reduce(out=square[:], in_=delta_sq[:], axis=AXIS.X, op=ALU.add)
+        apart = keep.tile([P, ROW_BLOCKS, SHIFTS], F32)
+        nc.vector.tensor_single_scalar(out=apart[:], in_=square[:], scalar=0.0, op=ALU.is_gt)
+        floored = keep.tile([P, ROW_BLOCKS, SHIFTS], F32)
+        nc.vector.tensor_scalar_max(out=floored[:], in0=square[:], scalar1=SMALLEST_SQUARE)
+        root = keep.tile([P, ROW_BLOCKS, SHIFTS], F32)
+        nc.scalar.activation(out=root[:], in_=floored[:], func=ACT.Sqrt)
+        dist = keep.tile([P, ROW_BLOCKS, SHIFTS], F32)
+        nc.vector.tensor_tensor(out=dist[:], in0=root[:], in1=apart[:], op=ALU.mult)
+
+        vectors_t = banks.tile([P, P], BF16, tag="bank")
+        nc.tensor.transpose(vectors_t[:], vectors[:], ident_bf16[:])
+        per_feature = keep.tile([P, 2 * F_BLOCKS], F32)
+        nc.vector.tensor_copy(out=per_feature[:], in_=vectors_t[:, 0 : 2 * F_BLOCKS])
+        w_dist = per_feature[:, 0:F_BLOCKS]
+        bias1 = per_feature[:, F_BLOCKS : 2 * F_BLOCKS]
+
+        be2_all = keep.tile([P, ROW_BLOCKS, M], F32)
+        nc.vector.tensor_copy(out=be2_all[:], in_=be2_rows[:].unsqueeze(1).to_broadcast([P, ROW_BLOCKS, M]))
+
+        states = keep.tile([P, STATE_COLS, PACK], BF16, align_bytes=64)
+        by_node = states[:, 0:COLS, :].rearrange("p (u b) t -> p u b t", b=GRAPHS)
+        for g in range(GRAPHS // 4):
+            x_t = banks.tile([P, PACK, P], BF16, tag="bank")
+            for t in range(PACK):
+                nc.tensor.transpose(x_t[:, t, :], x_rows[:, g, t * P : (t + 1) * P], ident_bf16[:])
+            nc.scalar.copy(
+                out=by_node[:, :, 4 * g : 4 * g + 4, :], in_=x_t[:].rearrange("p t (bl u) -> p u bl t", u=NODES)
+            )
+        nc.vector.tensor_copy(out=states[:, COLS:COPY_COLS, :], in_=states[:, 0:COLS, :])
+        nc.vector.tensor_copy(out=states[:, COPY_COLS:STATE_COLS, :], in_=states[:, 0 : STATE_COLS - COPY_COLS, :])
+        x_words = keep.tile([P, COPIES, COPY_COLS], U32, align_bytes=64)
+        x_scales = keep.tile([P, COPIES, COPY_COLS], U8, align_bytes=64)
+
+        def quantise_states(copy):
+            first = copy * GRAPHS
+            nc.vector.quantize_mx(
+                out=x_words[:, copy, :].bitcast(FP8X4),
+                scales=x_scales[:, copy, :],
+                in_=states[:, first : first + COPY_COLS, :].rearrange("p w t -> p (w t)"),
+            )
+
+        quantise_states(0)
+
+        w1_words = keep.tile([P, 2, F], U32, align_bytes=64)
+        w1_scales = keep.tile([P, 2, F], U8, align_bytes=64)
+        for c in range(F_PASSES):
+            f_half = slice(c * K_PASS, (c + 1) * K_PASS)
+            for side, engine_copy in ((0, nc.vector.tensor_copy), (1, nc.scalar.copy)):
+                w1_grouped = stage.tile([P, K_PASS, PACK], BF16, align_bytes=64, bufs=4)
+                regroup(engine_copy, w1_grouped[:], w1_rows[:, side * PACK : (side + 1) * PACK, f_half])
+                nc.vector.quantize_mx(
+                    out=w1_words[:, side, f_half].bitcast(FP8X4),
+                    scales=w1_scales[:, side, f_half],
+                    in_=w1_grouped[:].rearrange("p w t -> p (w t)"),
+                )
+        w2_grouped = keep.tile([P, F_PASSES, M, PACK], BF16, align_bytes=64)
+        for c in range(F_PASSES):
+            regroup(nc.vector.tensor_copy, w2_grouped[:, c], w2_rows[:, c * PACK : (c + 1) * PACK, :])
+        w2_words = keep.tile([P, F_PASSES * M], U32, align_bytes=64)
+        w2_scales = keep.tile([P, F_PASSES * M], U8, align_bytes=64)
+        nc.vector.quantize_mx(
+            out=w2_words[:].bitcast(FP8X4),
+            scales=w2_scales[:],
+            in_=w2_grouped[:].rearrange("p c m t -> p (c m t)"),
+        )
+
+        def distance_term(shift):
+            if 0 < shift < COPIES:
+                quantise_states(shift)
+            spread = banks.tile([P, ROW_BLOCKS, P], F32, tag="bank")
+            for q in range(ROW_BLOCKS):
+                nc.tensor.transpose(spread[:, q, :], dist[:, q, shift : shift + 1].to_broadcast([P, P]), ident_f32[:])
+            dist_row = stage.tile([P, COLS], F32)
+            nc.scalar.copy(out=dist_row[:], in_=spread[:].rearrange("p q k -> p (q k)"))
+            term = stage.tile([P, F_BLOCKS, COLS], F32)
+            for j in range(F_BLOCKS):
+                nc.gpsimd.tensor_scalar(
+                    out=term[:, j, :],
+                    in0=dist_row[:],
+                    scalar1=w_dist[:, j : j + 1],
+                    scalar2=bias1[:, j : j + 1],
+                    op0=ALU.mult,
+                    op1=ALU.add,
+                )
+            return term
+
+        def hidden(shift, swapped, c, term):
+            window = slice((shift // COPIES) * WINDOW_STEP, (shift // COPIES) * WINDOW_STEP + COLS)
+            own = (x_words[:, 0, 0:COLS], x_scales[:, 0, 0:COLS])
+            partner = (x_words[:, shift % COPIES, window], x_scales[:, shift % COPIES, window])
+            senders = (partner, own) if swapped else (own, partner)
+            pre = work.tile([P, PACK, COLS], F32)
+            for t in range(PACK):
+                j = c * PACK + t
+                f_cols = slice(j * P, (j + 1) * P)
+                acc = banks.tile([P, COLS], F32, tag="bank")
+                for side in range(2):
+                    nc.tensor.matmul_mx(
+                        out=acc[:],
+                        lhsT=w1_words[:, side, f_cols].bitcast(FP8X4),
+                        lhsT_scale=w1_scales[:, side, f_cols],
+                        rhs=senders[side][0].bitcast(FP8X4),
+                        rhs_scale=senders[side][1],
+                        start=(side == 0),
+                        stop=(side == 1),
+                    )
+                nc.vector.tensor_tensor(out=pre[:, t, :], in0=acc[:], in1=term[:, j, :], op=ALU.add)
+            h = work.tile([P, COLS, PACK], BF16, align_bytes=64)
+            nc.scalar.activation(
+                out=h[:].rearrange("p (g i) t -> p g t i", i=4),
+                in_=pre[:].rearrange("p t (g i) -> p g t i", i=4),
+                func=ACT.Silu,
+            )
+            return h
+
+        def quantise_hidden(h, h_words, h_scales, c):
+            nc.vector.quantize_mx(
+                out=h_words[:, c, :].bitcast(FP8X4),
+                scales=h_scales[:, c, :],
+                in_=h[:].rearrange("p w t -> p (w t)"),
+            )
+
+        out_rows = out.rearrange("b i j m -> b (i j) m")
+
+        def messages(shift, swapped, h_words, h_scales):
+            msg = msg_banks.tile([P, ROW_BLOCKS, M], F32)
+            for q in range(ROW_BLOCKS):
+                edges = slice(q * P, (q + 1) * P)
+                for c in range(F_PASSES):
+                    nc.tensor.matmul_mx(
+                        out=msg[:, q, :],
+                        lhsT=h_words[:, c, edges].bitcast(FP8X4),
+                        lhsT_scale=h_scales[:, c, edges],
+                        rhs=w2_words[:, c * M : (c + 1) * M].bitcast(FP8X4),
+                        rhs_scale=w2_scales[:, c * M : (c + 1) * M],
+                        start=(c == 0),
+                        stop=(c == F_PASSES - 1),
+                    )
+            result = work.tile([P, ROW_BLOCKS, M], F32, bufs=4)
+            nc.vector.tensor_tensor(out=result[:], in0=msg[:], in1=be2_all[:], op=ALU.add)
+            row_step = BLOCK_NODES * (NODES + 1)
+            for lane in range(BLOCK_NODES):
+                rows = slice(lane * GRAPHS, (lane + 1) * GRAPHS)
+                straight = (NODES - 1 - lane - shift) // BLOCK_NODES + 1
+                for q0, q1, v_minus_u in ((0, straight, shift), (straight, ROW_BLOCKS, shift - NODES)):
+                    if q1 > q0:
+                        first = (q0 * BLOCK_NODES + lane) * (NODES + 1) + v_minus_u * (NODES if swapped else 1)
+                        last = first + (q1 - q0 - 1) * row_step
+                        nc.sync.dma_start(out=out_rows[:, first : last + 1 : row_step, :], in_=result[rows, q0:q1, :])
+
+        tiles = []
+        for shift in range(SHIFTS):
+            tiles.append((shift, False))
+            if 0 < shift < SHIFTS - 1:
+                tiles.append((shift, True))
+
+        next_term = distance_term(0)
+        unquantised = None
+        complete = None
+        for shift, swapped in tiles:
+            if not swapped:
+                term = next_term
+                if shift + 1 < SHIFTS:
+                    next_term = distance_term(shift + 1)
+            h_words = work.tile([P, F_PASSES, COLS], U32, align_bytes=64)
+            h_scales = work.tile([P, F_PASSES, COLS], U8, align_bytes=64)
+            for c in range(F_PASSES):
+                h = hidden(shift, swapped, c, term)
+                if unquantised is not None:
+                    quantise_hidden(*unquantised)
+                unquantised = (h, h_words, h_scales, c)
+                if c == F_PASSES - 1 and complete is not None:
+                    messages(*complete)
+            complete = (shift, swapped, h_words, h_scales)
+        quantise_hidden(*unquantised)
+        messages(*complete)

@@ -243,8 +243,10 @@ def tile_graphmessagelayer_pa_t_kernel(tc, node_state, positions, We1, be1, We2,
                         start=(c == 0),
                         stop=(c == F_PASSES - 1),
                     )
+            product = work.tile([P, ROW_BLOCKS, M], F32)
+            nc.scalar.copy(out=product[:], in_=msg[:])
             result = work.tile([P, ROW_BLOCKS, M], F32, bufs=4)
-            nc.vector.tensor_tensor(out=result[:], in0=msg[:], in1=be2_all[:], op=ALU.add)
+            nc.gpsimd.tensor_tensor(out=result[:], in0=product[:], in1=be2_all[:], op=ALU.add)
             row_step = BLOCK_NODES * (NODES + 1)
             for lane in range(BLOCK_NODES):
                 rows = slice(lane * GRAPHS, (lane + 1) * GRAPHS)

@@ -38,6 +38,9 @@ STATE_COLS = COPY_COLS + (COPIES - 1) * GRAPHS
 REACH = (ROW_BLOCKS - 1) * BLOCK_NODES + SHIFTS
 SMALLEST_SQUARE = 2.0**-100
 
+QUANTISE_LAG = 2
+MESSAGE_LAG = 4
+
 FLOPS = 2 * GRAPHS * NODES * H * 2 * F + 2 * GRAPHS * NODES * NODES * F * M
 
 
@@ -171,25 +174,23 @@ def tile_graphmessagelayer_pa_t_kernel(tc, node_state, positions, We1, be1, We2,
             in_=w2_grouped[:].rearrange("p c m t -> p (c m t)"),
         )
 
-        def distance_term(shift):
-            if 0 < shift < COPIES:
-                quantise_states(shift)
+        def spread_distances(shift):
             spread = banks.tile([P, ROW_BLOCKS, P], F32, tag="bank")
             for q in range(ROW_BLOCKS):
                 nc.tensor.transpose(spread[:, q, :], dist[:, q, shift : shift + 1].to_broadcast([P, P]), ident_f32[:])
             dist_row = stage.tile([P, COLS], F32)
             nc.scalar.copy(out=dist_row[:], in_=spread[:].rearrange("p q k -> p (q k)"))
-            term = stage.tile([P, F_BLOCKS, COLS], F32)
-            for j in range(F_BLOCKS):
-                nc.gpsimd.tensor_scalar(
-                    out=term[:, j, :],
-                    in0=dist_row[:],
-                    scalar1=w_dist[:, j : j + 1],
-                    scalar2=bias1[:, j : j + 1],
-                    op0=ALU.mult,
-                    op1=ALU.add,
-                )
-            return term
+            return dist_row
+
+        def distance_term(term, dist_row, j):
+            nc.gpsimd.tensor_scalar(
+                out=term[:, j, :],
+                in0=dist_row[:],
+                scalar1=w_dist[:, j : j + 1],
+                scalar2=bias1[:, j : j + 1],
+                op0=ALU.mult,
+                op1=ALU.add,
+            )
 
         def hidden(shift, swapped, c, term):
             window = slice((shift // COPIES) * WINDOW_STEP, (shift // COPIES) * WINDOW_STEP + COLS)
@@ -212,20 +213,13 @@ def tile_graphmessagelayer_pa_t_kernel(tc, node_state, positions, We1, be1, We2,
                         stop=(side == 1),
                     )
                 nc.vector.tensor_tensor(out=pre[:, t, :], in0=acc[:], in1=term[:, j, :], op=ALU.add)
-            h = work.tile([P, COLS, PACK], BF16, align_bytes=64)
+            h = work.tile([P, COLS, PACK], BF16, align_bytes=64, bufs=QUANTISE_LAG + 2)
             nc.scalar.activation(
                 out=h[:].rearrange("p (g i) t -> p g t i", i=4),
                 in_=pre[:].rearrange("p t (g i) -> p g t i", i=4),
                 func=ACT.Silu,
             )
             return h
-
-        def quantise_hidden(h, h_words, h_scales, c):
-            nc.vector.quantize_mx(
-                out=h_words[:, c, :].bitcast(FP8X4),
-                scales=h_scales[:, c, :],
-                in_=h[:].rearrange("p w t -> p (w t)"),
-            )
 
         out_rows = out.rearrange("b i j m -> b (i j) m")
 
@@ -257,29 +251,51 @@ def tile_graphmessagelayer_pa_t_kernel(tc, node_state, positions, We1, be1, We2,
                         last = first + (q1 - q0 - 1) * row_step
                         nc.sync.dma_start(out=out_rows[:, first : last + 1 : row_step, :], in_=result[rows, q0:q1, :])
 
-        tiles = []
-        for shift in range(SHIFTS):
-            tiles.append((shift, False))
-            if 0 < shift < SHIFTS - 1:
-                tiles.append((shift, True))
+        steps = []
+        for shift in reversed(range(SHIFTS)):
+            directions = (False, True) if 0 < shift < SHIFTS - 1 else (False,)
+            halves = [(swapped, c) for swapped in directions for c in range(F_PASSES)]
+            share = F_BLOCKS // len(halves)
+            for k, (swapped, c) in enumerate(halves):
+                steps.append((shift, swapped, c, k * share, share))
 
-        next_term = distance_term(0)
-        unquantised = None
-        complete = None
-        for shift, swapped in tiles:
-            if not swapped:
-                term = next_term
-                if shift + 1 < SHIFTS:
-                    next_term = distance_term(shift + 1)
-            h_words = work.tile([P, F_PASSES, COLS], U32, align_bytes=64)
-            h_scales = work.tile([P, F_PASSES, COLS], U8, align_bytes=64)
-            for c in range(F_PASSES):
-                h = hidden(shift, swapped, c, term)
-                if unquantised is not None:
-                    quantise_hidden(*unquantised)
-                unquantised = (h, h_words, h_scales, c)
-                if c == F_PASSES - 1 and complete is not None:
-                    messages(*complete)
-            complete = (shift, swapped, h_words, h_scales)
-        quantise_hidden(*unquantised)
-        messages(*complete)
+        terms = {}
+        rows_of = {}
+        hs = {}
+        codes = {}
+
+        rows_of[SHIFTS - 1] = spread_distances(SHIFTS - 1)
+        first_term = stage.tile([P, F_BLOCKS, COLS], F32, tag="term")
+        terms[SHIFTS - 1] = first_term
+        for j in range(F_BLOCKS):
+            distance_term(first_term, rows_of[SHIFTS - 1], j)
+
+        with tc.manual_schedule():
+            for g in range(len(steps) + MESSAGE_LAG):
+                if g < len(steps):
+                    shift, swapped, c, first_block, share = steps[g]
+                    if shift > 0:
+                        if first_block == 0:
+                            if shift - 1 > SHIFTS - 1 - COPIES:
+                                quantise_states((shift - 1) % COPIES)
+                            rows_of[shift - 1] = spread_distances(shift - 1)
+                            next_term = stage.tile([P, F_BLOCKS, COLS], F32, tag="term")
+                            terms[shift - 1] = next_term
+                        for j in range(first_block, first_block + share):
+                            distance_term(terms[shift - 1], rows_of[shift - 1], j)
+                    hs[g] = hidden(shift, swapped, c, terms[shift])
+                    if c == 0:
+                        h_words = work.tile([P, F_PASSES, COLS], U32, align_bytes=64, bufs=4)
+                        h_scales = work.tile([P, F_PASSES, COLS], U8, align_bytes=64, bufs=4)
+                        codes[g // F_PASSES] = (h_words, h_scales)
+                ready = g - QUANTISE_LAG
+                if 0 <= ready < len(steps):
+                    h_words, h_scales = codes[ready // F_PASSES]
+                    nc.vector.quantize_mx(
+                        out=h_words[:, steps[ready][2], :].bitcast(FP8X4),
+                        scales=h_scales[:, steps[ready][2], :],
+                        in_=hs[ready][:].rearrange("p w t -> p (w t)"),
+                    )
+                done = g - MESSAGE_LAG
+                if done >= 0 and steps[done][2] == F_PASSES - 1:
+                    messages(steps[done][0], steps[done][1], *codes[done // F_PASSES])

@@ -38,6 +38,7 @@ STATE_COLS = COPY_COLS + (COPIES - 1) * GRAPHS
 REACH = (ROW_BLOCKS - 1) * BLOCK_NODES + SHIFTS
 SMALLEST_SQUARE = 2.0**-100
 
+LINE = 4
 QUANTISE_LAG = 2
 MESSAGE_LAG = 4
 
@@ -197,7 +198,7 @@ def tile_graphmessagelayer_pa_t_kernel(tc, node_state, positions, We1, be1, We2,
             own = (x_words[:, 0, 0:COLS], x_scales[:, 0, 0:COLS])
             partner = (x_words[:, shift % COPIES, window], x_scales[:, shift % COPIES, window])
             senders = (partner, own) if swapped else (own, partner)
-            pre = work.tile([P, PACK, COLS], F32)
+            pre = work.tile([P, COLS // LINE, PACK, LINE], F32)
             for t in range(PACK):
                 j = c * PACK + t
                 f_cols = slice(j * P, (j + 1) * P)
@@ -212,13 +213,14 @@ def tile_graphmessagelayer_pa_t_kernel(tc, node_state, positions, We1, be1, We2,
                         start=(side == 0),
                         stop=(side == 1),
                     )
-                nc.vector.tensor_tensor(out=pre[:, t, :], in0=acc[:], in1=term[:, j, :], op=ALU.add)
+                nc.vector.tensor_tensor(
+                    out=pre[:, :, t, :],
+                    in0=acc[:].rearrange("p (g i) -> p g i", i=LINE),
+                    in1=term[:, j, :].rearrange("p (g i) -> p g i", i=LINE),
+                    op=ALU.add,
+                )
             h = work.tile([P, COLS, PACK], BF16, align_bytes=64, bufs=QUANTISE_LAG + 2)
-            nc.scalar.activation(
-                out=h[:].rearrange("p (g i) t -> p g t i", i=4),
-                in_=pre[:].rearrange("p t (g i) -> p g t i", i=4),
-                func=ACT.Silu,
-            )
+            nc.scalar.activation(out=h[:].rearrange("p (g i) t -> p g t i", i=LINE), in_=pre[:], func=ACT.Silu)
             return h
 
         out_rows = out.rearrange("b i j m -> b (i j) m")

@@ -193,7 +193,7 @@ def tile_graphmessagelayer_pa_t_kernel(tc, node_state, positions, We1, be1, We2,
                 op1=ALU.add,
             )
 
-        def hidden(shift, swapped, c, term):
+        def hidden(shift, swapped, c, term, h):
             window = slice((shift // COPIES) * WINDOW_STEP, (shift // COPIES) * WINDOW_STEP + COLS)
             own = (x_words[:, 0, 0:COLS], x_scales[:, 0, 0:COLS])
             partner = (x_words[:, shift % COPIES, window], x_scales[:, shift % COPIES, window])
@@ -219,9 +219,7 @@ def tile_graphmessagelayer_pa_t_kernel(tc, node_state, positions, We1, be1, We2,
                     in1=term[:, j, :].rearrange("p (g i) -> p g i", i=LINE),
                     op=ALU.add,
                 )
-            h = work.tile([P, COLS, PACK], BF16, align_bytes=64, bufs=QUANTISE_LAG + 2)
-            nc.scalar.activation(out=h[:].rearrange("p (g i) t -> p g t i", i=LINE), in_=pre[:], func=ACT.Silu)
-            return h
+            nc.scalar.activation(out=h[:, c].rearrange("p (g i) t -> p g t i", i=LINE), in_=pre[:], func=ACT.Silu)
 
         out_rows = out.rearrange("b i j m -> b (i j) m")
 
@@ -285,18 +283,20 @@ def tile_graphmessagelayer_pa_t_kernel(tc, node_state, positions, We1, be1, We2,
                             terms[shift - 1] = next_term
                         for j in range(first_block, first_block + share):
                             distance_term(terms[shift - 1], rows_of[shift - 1], j)
-                    hs[g] = hidden(shift, swapped, c, terms[shift])
                     if c == 0:
+                        h = work.tile([P, F_PASSES, COLS, PACK], BF16, align_bytes=64)
+                        hs[g // F_PASSES] = h
                         h_words = work.tile([P, F_PASSES, COLS], U32, align_bytes=64, bufs=4)
                         h_scales = work.tile([P, F_PASSES, COLS], U8, align_bytes=64, bufs=4)
                         codes[g // F_PASSES] = (h_words, h_scales)
+                    hidden(shift, swapped, c, terms[shift], hs[g // F_PASSES])
                 ready = g - QUANTISE_LAG
-                if 0 <= ready < len(steps):
+                if 0 <= ready < len(steps) and steps[ready][2] == F_PASSES - 1:
                     h_words, h_scales = codes[ready // F_PASSES]
                     nc.vector.quantize_mx(
-                        out=h_words[:, steps[ready][2], :].bitcast(FP8X4),
-                        scales=h_scales[:, steps[ready][2], :],
-                        in_=hs[ready][:].rearrange("p w t -> p (w t)"),
+                        out=h_words[:].rearrange("p c w -> p (c w)").bitcast(FP8X4),
+                        scales=h_scales[:].rearrange("p c w -> p (c w)"),
+                        in_=hs[ready // F_PASSES][:].rearrange("p c w t -> p (c w t)"),
                     )
                 done = g - MESSAGE_LAG
                 if done >= 0 and steps[done][2] == F_PASSES - 1:

@@ -28,17 +28,20 @@ F_BLOCKS = F // P
 F_PASSES = F // K_PASS
 ROW_BLOCKS = COLS // P
 BLOCK_NODES = P // GRAPHS
-SHIFTS = NODES // 2 + 1
+MAX_SHIFT = NODES // 2
 
 COPIES = 4
 WINDOW_STEP = COPIES * GRAPHS
-COPY_COLS = 2 * COLS
+AHEAD_COLS = MAX_SHIFT // COPIES * WINDOW_STEP
+COPY_COLS = COLS + AHEAD_COLS
 STATE_COLS = COPY_COLS + (COPIES - 1) * GRAPHS
 
-REACH = (ROW_BLOCKS - 1) * BLOCK_NODES + SHIFTS
+REACH = (ROW_BLOCKS - 1) * BLOCK_NODES + MAX_SHIFT + 1
 SMALLEST_SQUARE = 2.0**-100
 
 LINE = 4
+PIECE = K_PASS // 2
+BE2_ROW = 32
 QUANTISE_LAG = 2
 MESSAGE_LAG = 4
 
@@ -60,6 +63,19 @@ def tile_graphmessagelayer_pa_t_kernel(tc, node_state, positions, We1, be1, We2,
         work = ctx.enter_context(tc.tile_pool(name="work", bufs=3))
         banks = ctx.enter_context(tc.psum_pool(name="banks", bufs=6))
         msg_banks = ctx.enter_context(tc.psum_pool(name="msg_banks", bufs=2))
+        ctx.enter_context(tc.manual_schedule())
+
+        vectors = keep.tile([P, P], BF16)
+        nc.vector.memset(vectors[:], 0.0)
+        pos_rows = keep.tile([P, 2, NODES * COORDS], BF16)
+        nc.vector.memset(pos_rows[:], 0.0)
+        for copy in range(2):
+            nc.scalar.dma_start(out=pos_rows[0:GRAPHS, copy, :], in_=positions.rearrange("b u c -> b (u c)"))
+        nc.scalar.dma_start(
+            out=vectors[0:F_BLOCKS, :], in_=We1[2 * H : 2 * H + 1, :].rearrange("o (j p) -> (o j) p", p=P)
+        )
+        nc.scalar.dma_start(out=vectors[F_BLOCKS : 2 * F_BLOCKS, :], in_=be1.rearrange("(j p) -> j p", p=P))
+        nc.scalar.dma_start(out=vectors[BE2_ROW : BE2_ROW + 1, :], in_=be2.unsqueeze(0))
 
         x_rows = keep.tile([P, GRAPHS // 4, H], BF16)
         nc.sync.dma_start(out=x_rows[:], in_=node_state.rearrange("(g bl) u k -> (bl u) g k", bl=4))
@@ -67,121 +83,161 @@ def tile_graphmessagelayer_pa_t_kernel(tc, node_state, positions, We1, be1, We2,
         w1_view = We1[0 : 2 * H, :].rearrange("(j p) f -> p j f", p=P)
         for c in range(F_PASSES):
             f_half = slice(c * K_PASS, (c + 1) * K_PASS)
-            nc.sync.dma_start(out=w1_rows[:, :, f_half], in_=w1_view[:, :, f_half])
+            for side in range(2):
+                blocks = slice(side * PACK, (side + 1) * PACK)
+                nc.sync.dma_start(out=w1_rows[:, blocks, f_half], in_=w1_view[:, blocks, f_half])
         w2_rows = keep.tile([P, F_BLOCKS, M], BF16)
         nc.sync.dma_start(out=w2_rows[:], in_=We2.rearrange("(j p) m -> p j m", p=P))
 
-        to_end = keep.tile([P, REACH, COORDS], BF16)
-        from_start = keep.tile([P, REACH, COORDS], BF16)
-        nc.vector.memset(to_end[:], 0.0)
-        nc.vector.memset(from_start[:], 0.0)
-        for lane in range(BLOCK_NODES):
-            rows = slice(lane * GRAPHS, (lane + 1) * GRAPHS)
-            left = NODES - lane
-            nc.scalar.dma_start(out=to_end[rows, 0:left, :], in_=positions[:, lane:NODES, :])
-            nc.scalar.dma_start(out=from_start[rows, left:REACH, :], in_=positions[:, 0 : REACH - left, :])
-        vectors = keep.tile([P, P], BF16)
-        nc.vector.memset(vectors[:], 0.0)
-        nc.scalar.dma_start(
-            out=vectors[0:F_BLOCKS, :], in_=We1[2 * H : 2 * H + 1, :].rearrange("o (j p) -> (o j) p", p=P)
-        )
-        nc.scalar.dma_start(out=vectors[F_BLOCKS : 2 * F_BLOCKS, :], in_=be1.rearrange("(j p) -> j p", p=P))
-        be2_rows = keep.tile([P, M], BF16)
-        nc.scalar.dma_start(out=be2_rows[:], in_=be2.partition_broadcast(P))
-
-        ident_bf16 = keep.tile([P, P], BF16)
-        make_identity(nc, ident_bf16[:])
+        left = P - GRAPHS
+        wide = keep.tile([P, left + P], BF16)
+        nc.vector.memset(wide[:, 0:left], 0.0)
+        make_identity(nc, wide[:, left : left + P])
+        ident_bf16 = wide[:, left : left + P]
         ident_f32 = keep.tile([P, P], F32)
         make_identity(nc, ident_f32[:])
+        one = keep.tile([P, 1], F32)
+        nc.vector.memset(one[:], 1.0)
+        warm = keep.tile([P, 1], F32)
+        nc.scalar.activation(out=warm[:], in_=one[:], func=ACT.Sqrt)
 
+        states = keep.tile([P, STATE_COLS, PACK], BF16, align_bytes=64)
+        by_node = states[:, 0:COLS, :].rearrange("p (u b) t -> p u b t", b=GRAPHS)
+
+        def turn_states(engine_copy, g):
+            x_t = banks.tile([P, PACK, P], BF16, tag="bank")
+            for t in range(PACK):
+                nc.tensor.transpose(x_t[:, t, :], x_rows[:, g, t * P : (t + 1) * P], ident_bf16)
+            engine_copy(
+                out=by_node[:, :, 4 * g : 4 * g + 4, :], in_=x_t[:].rearrange("p t (bl u) -> p u bl t", u=NODES)
+            )
+
+        by_vector = nc.vector.tensor_copy
+        by_scalar = nc.scalar.copy
+        turn_states(by_vector, 0)
+        turn_states(by_scalar, 1)
+        turn_states(by_vector, 2)
+        x_words = keep.tile([P, COPIES, COPY_COLS], U32, align_bytes=64)
+        x_scales = keep.tile([P, COPIES, COPY_COLS], U8, align_bytes=64)
+
+        def quantise_states(copy, cols):
+            first = copy * GRAPHS
+            nc.vector.quantize_mx(
+                out=x_words[:, copy, cols].bitcast(FP8X4),
+                scales=x_scales[:, copy, cols],
+                in_=states[:, first + cols.start : first + cols.stop, :].rearrange("p w t -> p (w t)"),
+            )
+
+        own_cols = slice(0, COLS)
+        ahead_cols = slice(COLS, COPY_COLS)
+
+        around_bank = banks.tile([P, REACH, COORDS], F32, tag="bank")
+        pos_round = pos_rows[:].rearrange("p r x -> p (r x)")
+        for lane in range(BLOCK_NODES):
+            nc.tensor.matmul(
+                around_bank[:].rearrange("p n x -> p (n x)"),
+                lhsT=wide[:, left - lane * GRAPHS : left - lane * GRAPHS + P],
+                rhs=pos_round[:, lane * COORDS : (lane + REACH) * COORDS],
+                start=(lane == 0),
+                stop=(lane == BLOCK_NODES - 1),
+            )
         around = keep.tile([P, REACH, COORDS], F32)
-        nc.vector.tensor_tensor(out=around[:], in0=to_end[:], in1=from_start[:], op=ALU.add)
-        delta = keep.tile([P, ROW_BLOCKS, SHIFTS, COORDS], F32)
+        nc.scalar.copy(out=around[:], in_=around_bank[:])
+        turn_states(by_scalar, 3)
+        vectors_t = banks.tile([P, P], BF16, tag="bank")
+        nc.tensor.transpose(vectors_t[:], vectors[:], ident_bf16)
+        be2_bank = msg_banks.tile([P, M], F32, tag="msg")
+        nc.tensor.matmul(
+            be2_bank[:],
+            lhsT=ident_bf16[:, BE2_ROW : BE2_ROW + 1].to_broadcast([P, P]),
+            rhs=vectors[:],
+            start=True,
+            stop=True,
+        )
+        per_feature = keep.tile([P, 2 * F_BLOCKS], F32)
+        nc.scalar.copy(out=per_feature[:], in_=vectors_t[:, 0 : 2 * F_BLOCKS])
+        w_dist = per_feature[:, 0:F_BLOCKS]
+        bias1 = per_feature[:, F_BLOCKS : 2 * F_BLOCKS]
+
+        w1_words = keep.tile([P, 2, F], U32, align_bytes=64)
+        w1_scales = keep.tile([P, 2, F], U8, align_bytes=64)
+
+        def regroup_w1(engine_copy, side, cols):
+            grouped = stage.tile([P, PIECE, PACK], BF16, align_bytes=64, bufs=8, tag="w1_grouped")
+            regroup(engine_copy, grouped[:], w1_rows[:, side * PACK : (side + 1) * PACK, cols])
+            return grouped
+
+        def quantise_w1(grouped, side, cols):
+            nc.vector.quantize_mx(
+                out=w1_words[:, side, cols].bitcast(FP8X4),
+                scales=w1_scales[:, side, cols],
+                in_=grouped[:].rearrange("p w t -> p (w t)"),
+            )
+
+        pieces = [slice(k * PIECE, (k + 1) * PIECE) for k in range(F // PIECE)]
+        g00 = regroup_w1(by_vector, 0, pieces[0])
+
+        delta = keep.tile([P, ROW_BLOCKS, MAX_SHIFT, COORDS], F32)
         for q in range(ROW_BLOCKS):
             first = q * BLOCK_NODES
             nc.vector.tensor_tensor(
                 out=delta[:, q],
-                in0=around[:, first : first + SHIFTS, :],
-                in1=around[:, first : first + 1, :].to_broadcast([P, SHIFTS, COORDS]),
+                in0=around[:, first + 1 : first + 1 + MAX_SHIFT, :],
+                in1=around[:, first : first + 1, :].to_broadcast([P, MAX_SHIFT, COORDS]),
                 op=ALU.subtract,
             )
-        delta_sq = keep.tile([P, ROW_BLOCKS, SHIFTS, COORDS], F32)
+        delta_sq = keep.tile([P, ROW_BLOCKS, MAX_SHIFT, COORDS], F32)
         nc.vector.tensor_tensor(out=delta_sq[:], in0=delta[:], in1=delta[:], op=ALU.mult)
-        square = keep.tile([P, ROW_BLOCKS, SHIFTS], F32)
+        square = keep.tile([P, ROW_BLOCKS, MAX_SHIFT], F32)
         nc.vector.tensor_reduce(out=square[:], in_=delta_sq[:], axis=AXIS.X, op=ALU.add)
-        apart = keep.tile([P, ROW_BLOCKS, SHIFTS], F32)
-        nc.vector.tensor_single_scalar(out=apart[:], in_=square[:], scalar=0.0, op=ALU.is_gt)
-        floored = keep.tile([P, ROW_BLOCKS, SHIFTS], F32)
+        floored = keep.tile([P, ROW_BLOCKS, MAX_SHIFT], F32)
         nc.vector.tensor_scalar_max(out=floored[:], in0=square[:], scalar1=SMALLEST_SQUARE)
-        root = keep.tile([P, ROW_BLOCKS, SHIFTS], F32)
-        nc.scalar.activation(out=root[:], in_=floored[:], func=ACT.Sqrt)
-        dist = keep.tile([P, ROW_BLOCKS, SHIFTS], F32)
-        nc.vector.tensor_tensor(out=dist[:], in0=root[:], in1=apart[:], op=ALU.mult)
+        apart = keep.tile([P, ROW_BLOCKS, MAX_SHIFT], F32)
+        nc.vector.tensor_single_scalar(out=apart[:], in_=square[:], scalar=0.0, op=ALU.is_gt)
 
-        vectors_t = banks.tile([P, P], BF16, tag="bank")
-        nc.tensor.transpose(vectors_t[:], vectors[:], ident_bf16[:])
-        per_feature = keep.tile([P, 2 * F_BLOCKS], F32)
-        nc.vector.tensor_copy(out=per_feature[:], in_=vectors_t[:, 0 : 2 * F_BLOCKS])
-        w_dist = per_feature[:, 0:F_BLOCKS]
-        bias1 = per_feature[:, F_BLOCKS : 2 * F_BLOCKS]
+        root = keep.tile([P, ROW_BLOCKS, MAX_SHIFT], F32)
+        nc.scalar.activation(out=root[:], in_=floored[:], func=ACT.Sqrt)
+        nc.scalar.activation(out=warm[:], in_=one[:], func=ACT.Silu)
+        g10 = regroup_w1(by_vector, 1, pieces[0])
+        dist = keep.tile([P, ROW_BLOCKS, MAX_SHIFT], F32)
+        nc.vector.tensor_tensor(out=dist[:], in0=root[:], in1=apart[:], op=ALU.mult)
+        quantise_states(0, own_cols)
+        quantise_w1(g00, 0, pieces[0])
+        quantise_w1(g10, 1, pieces[0])
+        g01 = regroup_w1(by_vector, 0, pieces[1])
+        g11 = regroup_w1(by_vector, 1, pieces[1])
+        quantise_w1(g01, 0, pieces[1])
+        quantise_w1(g11, 1, pieces[1])
 
         be2_all = keep.tile([P, ROW_BLOCKS, M], F32)
-        nc.vector.tensor_copy(out=be2_all[:], in_=be2_rows[:].unsqueeze(1).to_broadcast([P, ROW_BLOCKS, M]))
-
-        states = keep.tile([P, STATE_COLS, PACK], BF16, align_bytes=64)
-        by_node = states[:, 0:COLS, :].rearrange("p (u b) t -> p u b t", b=GRAPHS)
-        for g in range(GRAPHS // 4):
-            x_t = banks.tile([P, PACK, P], BF16, tag="bank")
-            for t in range(PACK):
-                nc.tensor.transpose(x_t[:, t, :], x_rows[:, g, t * P : (t + 1) * P], ident_bf16[:])
-            nc.scalar.copy(
-                out=by_node[:, :, 4 * g : 4 * g + 4, :], in_=x_t[:].rearrange("p t (bl u) -> p u bl t", u=NODES)
-            )
-        nc.vector.tensor_copy(out=states[:, COLS:COPY_COLS, :], in_=states[:, 0:COLS, :])
-        nc.vector.tensor_copy(out=states[:, COPY_COLS:STATE_COLS, :], in_=states[:, 0 : STATE_COLS - COPY_COLS, :])
-        x_words = keep.tile([P, COPIES, COPY_COLS], U32, align_bytes=64)
-        x_scales = keep.tile([P, COPIES, COPY_COLS], U8, align_bytes=64)
-
-        def quantise_states(copy):
-            first = copy * GRAPHS
-            nc.vector.quantize_mx(
-                out=x_words[:, copy, :].bitcast(FP8X4),
-                scales=x_scales[:, copy, :],
-                in_=states[:, first : first + COPY_COLS, :].rearrange("p w t -> p (w t)"),
-            )
-
-        quantise_states(0)
-
-        w1_words = keep.tile([P, 2, F], U32, align_bytes=64)
-        w1_scales = keep.tile([P, 2, F], U8, align_bytes=64)
-        for c in range(F_PASSES):
-            f_half = slice(c * K_PASS, (c + 1) * K_PASS)
-            for side, engine_copy in ((0, nc.vector.tensor_copy), (1, nc.scalar.copy)):
-                w1_grouped = stage.tile([P, K_PASS, PACK], BF16, align_bytes=64, bufs=4)
-                regroup(engine_copy, w1_grouped[:], w1_rows[:, side * PACK : (side + 1) * PACK, f_half])
-                nc.vector.quantize_mx(
-                    out=w1_words[:, side, f_half].bitcast(FP8X4),
-                    scales=w1_scales[:, side, f_half],
-                    in_=w1_grouped[:].rearrange("p w t -> p (w t)"),
-                )
         w2_grouped = keep.tile([P, F_PASSES, M, PACK], BF16, align_bytes=64)
-        for c in range(F_PASSES):
-            regroup(nc.vector.tensor_copy, w2_grouped[:, c], w2_rows[:, c * PACK : (c + 1) * PACK, :])
         w2_words = keep.tile([P, F_PASSES * M], U32, align_bytes=64)
         w2_scales = keep.tile([P, F_PASSES * M], U8, align_bytes=64)
-        nc.vector.quantize_mx(
-            out=w2_words[:].bitcast(FP8X4),
-            scales=w2_scales[:],
-            in_=w2_grouped[:].rearrange("p c m t -> p (c m t)"),
-        )
+
+        def prepare_w2():
+            for c in range(F_PASSES):
+                regroup(nc.vector.tensor_copy, w2_grouped[:, c], w2_rows[:, c * PACK : (c + 1) * PACK, :])
+            nc.vector.quantize_mx(
+                out=w2_words[:].bitcast(FP8X4),
+                scales=w2_scales[:],
+                in_=w2_grouped[:].rearrange("p c m t -> p (c m t)"),
+            )
 
         def spread_distances(shift):
             spread = banks.tile([P, ROW_BLOCKS, P], F32, tag="bank")
             for q in range(ROW_BLOCKS):
-                nc.tensor.transpose(spread[:, q, :], dist[:, q, shift : shift + 1].to_broadcast([P, P]), ident_f32[:])
+                nc.tensor.transpose(spread[:, q, :], dist[:, q, shift - 1 : shift].to_broadcast([P, P]), ident_f32[:])
             dist_row = stage.tile([P, COLS], F32)
             nc.scalar.copy(out=dist_row[:], in_=spread[:].rearrange("p q k -> p (q k)"))
             return dist_row
+
+        terms = {}
+        rows_of = {}
+
+        def start_term(shift):
+            rows_of[shift] = spread_distances(shift)
+            next_term = stage.tile([P, F_BLOCKS, COLS], F32, tag="term")
+            terms[shift] = next_term
 
         def distance_term(term, dist_row, j):
             nc.gpsimd.tensor_scalar(
@@ -193,12 +249,12 @@ def tile_graphmessagelayer_pa_t_kernel(tc, node_state, positions, We1, be1, We2,
                 op1=ALU.add,
             )
 
-        def hidden(shift, swapped, c, term, h):
+        def node_terms(shift, swapped, c):
             window = slice((shift // COPIES) * WINDOW_STEP, (shift // COPIES) * WINDOW_STEP + COLS)
             own = (x_words[:, 0, 0:COLS], x_scales[:, 0, 0:COLS])
             partner = (x_words[:, shift % COPIES, window], x_scales[:, shift % COPIES, window])
             senders = (partner, own) if swapped else (own, partner)
-            pre = work.tile([P, COLS // LINE, PACK, LINE], F32)
+            accs = []
             for t in range(PACK):
                 j = c * PACK + t
                 f_cols = slice(j * P, (j + 1) * P)
@@ -213,23 +269,51 @@ def tile_graphmessagelayer_pa_t_kernel(tc, node_state, positions, We1, be1, We2,
                         start=(side == 0),
                         stop=(side == 1),
                     )
+                accs.append(acc)
+            return accs
+
+        def lines(plane):
+            return plane.rearrange("p (g i) -> p g i", i=LINE)
+
+        def add_terms(pre, accs, term, c, cols):
+            groups = slice(cols.start // LINE, cols.stop // LINE)
+            for t in range(PACK):
                 nc.vector.tensor_tensor(
-                    out=pre[:, :, t, :],
-                    in0=acc[:].rearrange("p (g i) -> p g i", i=LINE),
-                    in1=term[:, j, :].rearrange("p (g i) -> p g i", i=LINE),
+                    out=pre[:, groups, t, :],
+                    in0=lines(accs[t][:, cols]),
+                    in1=lines(term[:, c * PACK + t, cols]),
                     op=ALU.add,
                 )
-            nc.scalar.activation(out=h[:, c].rearrange("p (g i) t -> p g t i", i=LINE), in_=pre[:], func=ACT.Silu)
 
-        out_rows = out.rearrange("b i j m -> b (i j) m")
+        def add_bias(pre, accs, c):
+            for t in range(PACK):
+                b_col = bias1[:, c * PACK + t : c * PACK + t + 1]
+                if t < PACK // 2:
+                    nc.vector.tensor_scalar_add(out=pre[:, :, t, :], in0=lines(accs[t][:]), scalar1=b_col)
+                else:
+                    nc.scalar.activation(
+                        out=pre[:, :, t, :], in_=lines(accs[t][:]), func=ACT.Identity, bias=b_col, scale=1.0
+                    )
 
-        def messages(shift, swapped, h_words, h_scales):
-            msg = msg_banks.tile([P, ROW_BLOCKS, M], F32)
-            for q in range(ROW_BLOCKS):
+        def apply_silu(h, pre, c, cols):
+            groups = slice(cols.start // LINE, cols.stop // LINE)
+            nc.scalar.activation(
+                out=h[:, c, cols, :].rearrange("p (g i) t -> p g t i", i=LINE), in_=pre[:, groups], func=ACT.Silu
+            )
+
+        def quantise_h(h, h_words, h_scales, c0, c1, cols):
+            nc.vector.quantize_mx(
+                out=h_words[:, c0:c1, cols].rearrange("p c w -> p (c w)").bitcast(FP8X4),
+                scales=h_scales[:, c0:c1, cols].rearrange("p c w -> p (c w)"),
+                in_=h[:, c0:c1, cols, :].rearrange("p c w t -> p (c w t)"),
+            )
+
+        def multiply_w2(msg, h_words, h_scales, q0, q1):
+            for q in range(q0, q1):
                 edges = slice(q * P, (q + 1) * P)
                 for c in range(F_PASSES):
                     nc.tensor.matmul_mx(
-                        out=msg[:, q, :],
+                        out=msg[:, q - q0, :],
                         lhsT=h_words[:, c, edges].bitcast(FP8X4),
                         lhsT_scale=h_scales[:, c, edges],
                         rhs=w2_words[:, c * M : (c + 1) * M].bitcast(FP8X4),
@@ -237,67 +321,118 @@ def tile_graphmessagelayer_pa_t_kernel(tc, node_state, positions, We1, be1, We2,
                         start=(c == 0),
                         stop=(c == F_PASSES - 1),
                     )
-            product = work.tile([P, ROW_BLOCKS, M], F32)
-            nc.scalar.copy(out=product[:], in_=msg[:])
-            result = work.tile([P, ROW_BLOCKS, M], F32, bufs=4)
-            nc.gpsimd.tensor_tensor(out=result[:], in0=product[:], in1=be2_all[:], op=ALU.add)
+
+        out_rows = out.rearrange("b i j m -> b (i j) m")
+
+        def store(result, shift, swapped, round_queue):
             row_step = BLOCK_NODES * (NODES + 1)
             for lane in range(BLOCK_NODES):
                 rows = slice(lane * GRAPHS, (lane + 1) * GRAPHS)
                 straight = (NODES - 1 - lane - shift) // BLOCK_NODES + 1
-                for q0, q1, v_minus_u in ((0, straight, shift), (straight, ROW_BLOCKS, shift - NODES)):
-                    if q1 > q0:
-                        first = (q0 * BLOCK_NODES + lane) * (NODES + 1) + v_minus_u * (NODES if swapped else 1)
-                        last = first + (q1 - q0 - 1) * row_step
-                        nc.sync.dma_start(out=out_rows[:, first : last + 1 : row_step, :], in_=result[rows, q0:q1, :])
+                for queue, b0, b1, v_minus_u in (
+                    (nc.sync, 0, straight, shift),
+                    (round_queue, straight, ROW_BLOCKS, shift - NODES),
+                ):
+                    if b1 > b0:
+                        first = (b0 * BLOCK_NODES + lane) * (NODES + 1) + v_minus_u * (NODES if swapped else 1)
+                        last = first + (b1 - b0 - 1) * row_step
+                        queue.dma_start(out=out_rows[:, first : last + 1 : row_step, :], in_=result[rows, b0:b1, :])
 
+        def messages(tile):
+            msg = msg_banks.tile([P, ROW_BLOCKS, M], F32, tag="msg")
+            multiply_w2(msg, *codes[tile], 0, ROW_BLOCKS)
+            result = work.tile([P, ROW_BLOCKS, M], F32, bufs=4)
+            if tile < last_tile - 2:
+                product = work.tile([P, ROW_BLOCKS, M], F32)
+                nc.scalar.copy(out=product[:], in_=msg[:])
+                nc.gpsimd.tensor_tensor(out=result[:], in0=product[:], in1=be2_all[:], op=ALU.add)
+            else:
+                nc.vector.tensor_tensor(out=result[:], in0=msg[:], in1=be2_all[:], op=ALU.add)
+            store(result, *steps[tile * F_PASSES][0:2], nc.sync)
+
+        order = [0, *range(MAX_SHIFT, 0, -1)]
         steps = []
-        for shift in reversed(range(SHIFTS)):
-            directions = (False, True) if 0 < shift < SHIFTS - 1 else (False,)
+        for shift, coming in zip(order, (*order[1:], 0)):
+            directions = (False, True) if 0 < shift < MAX_SHIFT else (False,)
             halves = [(swapped, c) for swapped in directions for c in range(F_PASSES)]
             share = F_BLOCKS // len(halves)
             for k, (swapped, c) in enumerate(halves):
-                steps.append((shift, swapped, c, k * share, share))
+                steps.append((shift, swapped, c, coming, k * share, share))
 
-        terms = {}
-        rows_of = {}
+        all_cols = slice(0, COLS)
+        halves_of_cols = (slice(0, COLS // 2), slice(COLS // 2, COLS))
         hs = {}
         codes = {}
+        last_step = len(steps) - 1
+        last_tile = last_step // F_PASSES
 
-        rows_of[SHIFTS - 1] = spread_distances(SHIFTS - 1)
-        first_term = stage.tile([P, F_BLOCKS, COLS], F32, tag="term")
-        terms[SHIFTS - 1] = first_term
-        for j in range(F_BLOCKS):
-            distance_term(first_term, rows_of[SHIFTS - 1], j)
-
-        with tc.manual_schedule():
-            for g in range(len(steps) + MESSAGE_LAG):
-                if g < len(steps):
-                    shift, swapped, c, first_block, share = steps[g]
-                    if shift > 0:
-                        if first_block == 0:
-                            if shift - 1 > SHIFTS - 1 - COPIES:
-                                quantise_states((shift - 1) % COPIES)
-                            rows_of[shift - 1] = spread_distances(shift - 1)
-                            next_term = stage.tile([P, F_BLOCKS, COLS], F32, tag="term")
-                            terms[shift - 1] = next_term
-                        for j in range(first_block, first_block + share):
-                            distance_term(terms[shift - 1], rows_of[shift - 1], j)
-                    if c == 0:
-                        h = work.tile([P, F_PASSES, COLS, PACK], BF16, align_bytes=64)
-                        hs[g // F_PASSES] = h
-                        h_words = work.tile([P, F_PASSES, COLS], U32, align_bytes=64, bufs=4)
-                        h_scales = work.tile([P, F_PASSES, COLS], U8, align_bytes=64, bufs=4)
-                        codes[g // F_PASSES] = (h_words, h_scales)
-                    hidden(shift, swapped, c, terms[shift], hs[g // F_PASSES])
-                ready = g - QUANTISE_LAG
-                if 0 <= ready < len(steps) and steps[ready][2] == F_PASSES - 1:
-                    h_words, h_scales = codes[ready // F_PASSES]
-                    nc.vector.quantize_mx(
-                        out=h_words[:].rearrange("p c w -> p (c w)").bitcast(FP8X4),
-                        scales=h_scales[:].rearrange("p c w -> p (c w)"),
-                        in_=hs[ready // F_PASSES][:].rearrange("p c w t -> p (c w t)"),
+        for g in range(len(steps)):
+            shift, swapped, c, coming, first_block, share = steps[g]
+            tile = g // F_PASSES
+            if c == 0:
+                h = work.tile([P, F_PASSES, COLS, PACK], BF16, align_bytes=64)
+                hs[tile] = h
+                h_words = work.tile([P, F_PASSES, COLS], U32, align_bytes=64, bufs=4)
+                h_scales = work.tile([P, F_PASSES, COLS], U8, align_bytes=64, bufs=4)
+                codes[tile] = (h_words, h_scales)
+            if coming > 0 and shift > 0:
+                if first_block == 0:
+                    if coming > MAX_SHIFT - COPIES:
+                        quantise_states(coming % COPIES, own_cols)
+                        quantise_states(coming % COPIES, ahead_cols)
+                    start_term(coming)
+                for j in range(first_block, first_block + share):
+                    distance_term(terms[coming], rows_of[coming], j)
+            pre = work.tile([P, COLS // LINE, PACK, LINE], F32)
+            if g == 0:
+                start_term(coming)
+            accs = node_terms(shift, swapped, c)
+            if shift == 0:
+                if c == 0:
+                    second_half = [
+                        (regroup_w1(engine_copy, side, cols), side, cols)
+                        for cols in pieces[2:4]
+                        for side, engine_copy in ((0, by_vector), (1, by_scalar))
+                    ]
+                for j in range(first_block, first_block + share):
+                    distance_term(terms[coming], rows_of[coming], j)
+                add_bias(pre, accs, c)
+                apply_silu(hs[tile], pre, c, all_cols)
+                if c == 0:
+                    for piece in second_half:
+                        quantise_w1(*piece)
+                    nc.vector.tensor_copy(
+                        out=states[:, COLS:STATE_COLS, :], in_=states[:, 0 : STATE_COLS - COLS, :]
                     )
-                done = g - MESSAGE_LAG
-                if done >= 0 and steps[done][2] == F_PASSES - 1:
-                    messages(steps[done][0], steps[done][1], *codes[done // F_PASSES])
+                    quantise_states(0, ahead_cols)
+                else:
+                    prepare_w2()
+                    nc.scalar.copy(out=be2_all[:], in_=be2_bank[:].unsqueeze(1).to_broadcast([P, ROW_BLOCKS, M]))
+            elif g < last_step:
+                add_terms(pre, accs, terms[shift], c, all_cols)
+                apply_silu(hs[tile], pre, c, all_cols)
+            else:
+                add_terms(pre, accs, terms[shift], c, halves_of_cols[0])
+                apply_silu(hs[tile], pre, c, halves_of_cols[0])
+                quantise_h(hs[tile - 1], *codes[tile - 1], 0, F_PASSES, all_cols)
+                add_terms(pre, accs, terms[shift], c, halves_of_cols[1])
+                apply_silu(hs[tile], pre, c, halves_of_cols[1])
+            ready = g - QUANTISE_LAG
+            if 0 <= ready < last_step - F_PASSES and steps[ready][2] == F_PASSES - 1:
+                tile = ready // F_PASSES
+                quantise_h(hs[tile], *codes[tile], 0, F_PASSES, all_cols)
+            done = g - MESSAGE_LAG
+            if 0 <= done and steps[done][2] == F_PASSES - 1:
+                messages(done // F_PASSES)
+
+        messages(last_tile - 1)
+        quantise_h(hs[last_tile], *codes[last_tile], 0, 1, all_cols)
+        result = work.tile([P, ROW_BLOCKS, M], F32, bufs=4)
+        for half, cols in enumerate(halves_of_cols):
+            q0 = half * ROW_BLOCKS // 2
+            q1 = q0 + ROW_BLOCKS // 2
+            quantise_h(hs[last_tile], *codes[last_tile], 1, 2, cols)
+            msg = banks.tile([P, ROW_BLOCKS // 2, M], F32, tag="bank")
+            multiply_w2(msg, *codes[last_tile], q0, q1)
+            nc.vector.tensor_tensor(out=result[:, q0:q1, :], in0=msg[:], in1=be2_all[:, q0:q1, :], op=ALU.add)
+        store(result, *steps[last_step][0:2], nc.gpsimd)

@@ -42,8 +42,8 @@ SMALLEST_SQUARE = 2.0**-100
 LINE = 4
 PIECE = K_PASS // 2
 BE2_ROW = 32
-QUANTISE_LAG = 2
-MESSAGE_LAG = 4
+QUANTISE_LAG = 3
+MESSAGE_LAG = 5
 
 FLOPS = 2 * GRAPHS * NODES * H * 2 * F + 2 * GRAPHS * NODES * NODES * F * M
 
@@ -239,6 +239,13 @@ def tile_graphmessagelayer_pa_t_kernel(tc, node_state, positions, We1, be1, We2,
             next_term = stage.tile([P, F_BLOCKS, COLS], F32, tag="term")
             terms[shift] = next_term
 
+        due = []
+
+        def make_due_terms():
+            for shift, j in due:
+                distance_term(terms[shift], rows_of[shift], j)
+            due.clear()
+
         def distance_term(term, dist_row, j):
             nc.gpsimd.tensor_scalar(
                 out=term[:, j, :],
@@ -341,14 +348,20 @@ def tile_graphmessagelayer_pa_t_kernel(tc, node_state, positions, We1, be1, We2,
         def messages(tile):
             msg = msg_banks.tile([P, ROW_BLOCKS, M], F32, tag="msg")
             multiply_w2(msg, *codes[tile], 0, ROW_BLOCKS)
-            result = work.tile([P, ROW_BLOCKS, M], F32, bufs=4)
-            if tile < last_tile - 2:
-                product = work.tile([P, ROW_BLOCKS, M], F32)
-                nc.scalar.copy(out=product[:], in_=msg[:])
+            product = work.tile([P, ROW_BLOCKS, M], F32)
+            nc.scalar.copy(out=product[:], in_=msg[:])
+            unfinished.append((product, tile))
+
+        unfinished = []
+
+        def finish_messages():
+            for product, tile in unfinished:
+                result = work.tile([P, ROW_BLOCKS, M], F32, bufs=4)
                 nc.gpsimd.tensor_tensor(out=result[:], in0=product[:], in1=be2_all[:], op=ALU.add)
-            else:
-                nc.vector.tensor_tensor(out=result[:], in0=msg[:], in1=be2_all[:], op=ALU.add)
-            store(result, *steps[tile * F_PASSES][0:2], nc.sync)
+                store(result, *steps[tile * F_PASSES][0:2], nc.sync)
+            unfinished.clear()
+
+        behind = keep.tile([P, LINE], U32)
 
         order = [0, *range(MAX_SHIFT, 0, -1)]
         steps = []
@@ -381,8 +394,10 @@ def tile_graphmessagelayer_pa_t_kernel(tc, node_state, positions, We1, be1, We2,
                         quantise_states(coming % COPIES, own_cols)
                         quantise_states(coming % COPIES, ahead_cols)
                     start_term(coming)
-                for j in range(first_block, first_block + share):
-                    distance_term(terms[coming], rows_of[coming], j)
+                if c == 0:
+                    due.extend([(coming, j) for j in range(first_block, first_block + F_PASSES * share)])
+                if shift == MAX_SHIFT:
+                    make_due_terms()
             pre = work.tile([P, COLS // LINE, PACK, LINE], F32)
             if g == 0:
                 start_term(coming)
@@ -394,8 +409,9 @@ def tile_graphmessagelayer_pa_t_kernel(tc, node_state, positions, We1, be1, We2,
                         for cols in pieces[2:4]
                         for side, engine_copy in ((0, by_vector), (1, by_scalar))
                     ]
-                for j in range(first_block, first_block + share):
-                    distance_term(terms[coming], rows_of[coming], j)
+                if c == 0:
+                    due.extend([(coming, j) for j in range(F_BLOCKS)])
+                make_due_terms()
                 add_bias(pre, accs, c)
                 apply_silu(hs[tile], pre, c, all_cols)
                 if c == 0:
@@ -415,17 +431,24 @@ def tile_graphmessagelayer_pa_t_kernel(tc, node_state, positions, We1, be1, We2,
                 add_terms(pre, accs, terms[shift], c, halves_of_cols[0])
                 apply_silu(hs[tile], pre, c, halves_of_cols[0])
                 quantise_h(hs[tile - 1], *codes[tile - 1], 0, F_PASSES, all_cols)
+                finish_messages()
+                messages(tile - 2)
+                finish_messages()
                 add_terms(pre, accs, terms[shift], c, halves_of_cols[1])
                 apply_silu(hs[tile], pre, c, halves_of_cols[1])
             ready = g - QUANTISE_LAG
-            if 0 <= ready < last_step - F_PASSES and steps[ready][2] == F_PASSES - 1:
+            if 0 <= ready and steps[ready][2] == F_PASSES - 1:
                 tile = ready // F_PASSES
                 quantise_h(hs[tile], *codes[tile], 0, F_PASSES, all_cols)
+                nc.gpsimd.tensor_copy(out=behind[:], in_=codes[tile][0][:, 0, 0:LINE])
+                make_due_terms()
+                finish_messages()
             done = g - MESSAGE_LAG
             if 0 <= done and steps[done][2] == F_PASSES - 1:
                 messages(done // F_PASSES)
 
         messages(last_tile - 1)
+        finish_messages()
         quantise_h(hs[last_tile], *codes[last_tile], 0, 1, all_cols)
         result = work.tile([P, ROW_BLOCKS, M], F32, bufs=4)
         for half, cols in enumerate(halves_of_cols):

@@ -39,6 +39,7 @@ STATE_COLS = COPY_COLS + (COPIES - 1) * GRAPHS
 REACH = (ROW_BLOCKS - 1) * BLOCK_NODES + MAX_SHIFT + 1
 SMALLEST_SQUARE = 2.0**-100
 
+SCALAR_BLOCKS = 1
 LINE = 4
 PIECE = K_PASS // 2
 BE2_ROW = 32
@@ -239,22 +240,14 @@ def tile_graphmessagelayer_pa_t_kernel(tc, node_state, positions, We1, be1, We2,
             next_term = stage.tile([P, F_BLOCKS, COLS], F32, tag="term")
             terms[shift] = next_term
 
-        due = []
-
-        def make_due_terms():
-            for shift, j in due:
-                distance_term(terms[shift], rows_of[shift], j)
-            due.clear()
-
         def distance_term(term, dist_row, j):
-            nc.gpsimd.tensor_scalar(
-                out=term[:, j, :],
-                in0=dist_row[:],
-                scalar1=w_dist[:, j : j + 1],
-                scalar2=bias1[:, j : j + 1],
-                op0=ALU.mult,
-                op1=ALU.add,
-            )
+            w_col, b_col = w_dist[:, j : j + 1], bias1[:, j : j + 1]
+            if j < SCALAR_BLOCKS:
+                nc.scalar.activation(out=term[:, j, :], in_=dist_row[:], func=ACT.Identity, scale=w_col, bias=b_col)
+            else:
+                nc.gpsimd.tensor_scalar(
+                    out=term[:, j, :], in0=dist_row[:], scalar1=w_col, scalar2=b_col, op0=ALU.mult, op1=ALU.add
+                )
 
         def node_terms(shift, swapped, c):
             window = slice((shift // COPIES) * WINDOW_STEP, (shift // COPIES) * WINDOW_STEP + COLS)
@@ -361,8 +354,6 @@ def tile_graphmessagelayer_pa_t_kernel(tc, node_state, positions, We1, be1, We2,
                 store(result, *steps[tile * F_PASSES][0:2], nc.sync)
             unfinished.clear()
 
-        behind = keep.tile([P, LINE], U32)
-
         order = [0, *range(MAX_SHIFT, 0, -1)]
         steps = []
         for shift, coming in zip(order, (*order[1:], 0)):
@@ -394,10 +385,8 @@ def tile_graphmessagelayer_pa_t_kernel(tc, node_state, positions, We1, be1, We2,
                         quantise_states(coming % COPIES, own_cols)
                         quantise_states(coming % COPIES, ahead_cols)
                     start_term(coming)
-                if c == 0:
-                    due.extend([(coming, j) for j in range(first_block, first_block + F_PASSES * share)])
-                if shift == MAX_SHIFT:
-                    make_due_terms()
+                for j in range(first_block, first_block + share):
+                    distance_term(terms[coming], rows_of[coming], j)
             pre = work.tile([P, COLS // LINE, PACK, LINE], F32)
             if g == 0:
                 start_term(coming)
@@ -409,9 +398,8 @@ def tile_graphmessagelayer_pa_t_kernel(tc, node_state, positions, We1, be1, We2,
                         for cols in pieces[2:4]
                         for side, engine_copy in ((0, by_vector), (1, by_scalar))
                     ]
-                if c == 0:
-                    due.extend([(coming, j) for j in range(F_BLOCKS)])
-                make_due_terms()
+                for j in range(first_block, first_block + share):
+                    distance_term(terms[coming], rows_of[coming], j)
                 add_bias(pre, accs, c)
                 apply_silu(hs[tile], pre, c, all_cols)
                 if c == 0:
@@ -428,28 +416,29 @@ def tile_graphmessagelayer_pa_t_kernel(tc, node_state, positions, We1, be1, We2,
                 add_terms(pre, accs, terms[shift], c, all_cols)
                 apply_silu(hs[tile], pre, c, all_cols)
             else:
-                add_terms(pre, accs, terms[shift], c, halves_of_cols[0])
-                apply_silu(hs[tile], pre, c, halves_of_cols[0])
-                quantise_h(hs[tile - 1], *codes[tile - 1], 0, F_PASSES, all_cols)
                 finish_messages()
                 messages(tile - 2)
                 finish_messages()
+                add_terms(pre, accs, terms[shift], c, halves_of_cols[0])
+                apply_silu(hs[tile], pre, c, halves_of_cols[0])
+                quantise_h(hs[tile - 1], *codes[tile - 1], 0, F_PASSES, all_cols)
                 add_terms(pre, accs, terms[shift], c, halves_of_cols[1])
                 apply_silu(hs[tile], pre, c, halves_of_cols[1])
             ready = g - QUANTISE_LAG
             if 0 <= ready and steps[ready][2] == F_PASSES - 1:
                 tile = ready // F_PASSES
                 quantise_h(hs[tile], *codes[tile], 0, F_PASSES, all_cols)
-                nc.gpsimd.tensor_copy(out=behind[:], in_=codes[tile][0][:, 0, 0:LINE])
-                make_due_terms()
-                finish_messages()
+            finish_messages()
             done = g - MESSAGE_LAG
             if 0 <= done and steps[done][2] == F_PASSES - 1:
                 messages(done // F_PASSES)
 
-        messages(last_tile - 1)
-        finish_messages()
+        msg = msg_banks.tile([P, ROW_BLOCKS, M], F32, tag="msg")
+        multiply_w2(msg, *codes[last_tile - 1], 0, ROW_BLOCKS)
         quantise_h(hs[last_tile], *codes[last_tile], 0, 1, all_cols)
+        result = work.tile([P, ROW_BLOCKS, M], F32, bufs=4)
+        nc.vector.tensor_tensor(out=result[:], in0=msg[:], in1=be2_all[:], op=ALU.add)
+        store(result, *steps[last_step - F_PASSES][0:2], nc.sync)
         result = work.tile([P, ROW_BLOCKS, M], F32, bufs=4)
         for half, cols in enumerate(halves_of_cols):
             q0 = half * ROW_BLOCKS // 2

@@ -40,10 +40,12 @@ REACH = (ROW_BLOCKS - 1) * BLOCK_NODES + MAX_SHIFT + 1
 SMALLEST_SQUARE = 2.0**-100
 
 SCALAR_BLOCKS = 1
+DIST_ROWS = MAX_SHIFT * ROW_BLOCKS
 LINE = 4
 PIECE = K_PASS // 2
 BE2_ROW = 32
 QUANTISE_LAG = 3
+ADD_LAG = 2
 MESSAGE_LAG = 5
 
 FLOPS = 2 * GRAPHS * NODES * H * 2 * F + 2 * GRAPHS * NODES * NODES * F * M
@@ -89,6 +91,9 @@ def tile_graphmessagelayer_pa_t_kernel(tc, node_state, positions, We1, be1, We2,
                 nc.sync.dma_start(out=w1_rows[:, blocks, f_half], in_=w1_view[:, blocks, f_half])
         w2_rows = keep.tile([P, F_BLOCKS, M], BF16)
         nc.sync.dma_start(out=w2_rows[:], in_=We2.rearrange("(j p) m -> p j m", p=P))
+
+        dist_square = keep.tile([P, P], F32)
+        nc.vector.memset(dist_square[:], 0.0)
 
         left = P - GRAPHS
         wide = keep.tile([P, left + P], BF16)
@@ -178,6 +183,7 @@ def tile_graphmessagelayer_pa_t_kernel(tc, node_state, positions, We1, be1, We2,
         pieces = [slice(k * PIECE, (k + 1) * PIECE) for k in range(F // PIECE)]
         g00 = regroup_w1(by_vector, 0, pieces[0])
 
+        dist = dist_square[:, 0:DIST_ROWS].rearrange("p (s q) -> p s q", q=ROW_BLOCKS)
         delta = keep.tile([P, ROW_BLOCKS, MAX_SHIFT, COORDS], F32)
         for q in range(ROW_BLOCKS):
             first = q * BLOCK_NODES
@@ -200,8 +206,7 @@ def tile_graphmessagelayer_pa_t_kernel(tc, node_state, positions, We1, be1, We2,
         nc.scalar.activation(out=root[:], in_=floored[:], func=ACT.Sqrt)
         nc.scalar.activation(out=warm[:], in_=one[:], func=ACT.Silu)
         g10 = regroup_w1(by_vector, 1, pieces[0])
-        dist = keep.tile([P, ROW_BLOCKS, MAX_SHIFT], F32)
-        nc.vector.tensor_tensor(out=dist[:], in0=root[:], in1=apart[:], op=ALU.mult)
+        nc.vector.tensor_tensor(out=dist.rearrange("p s q -> p q s"), in0=root[:], in1=apart[:], op=ALU.mult)
         quantise_states(0, own_cols)
         quantise_w1(g00, 0, pieces[0])
         quantise_w1(g10, 1, pieces[0])
@@ -224,29 +229,42 @@ def tile_graphmessagelayer_pa_t_kernel(tc, node_state, positions, We1, be1, We2,
                 in_=w2_grouped[:].rearrange("p c m t -> p (c m t)"),
             )
 
+        dist_rows = keep.tile([P, MAX_SHIFT, COLS], F32)
+
         def spread_distances(shift):
             spread = banks.tile([P, ROW_BLOCKS, P], F32, tag="bank")
             for q in range(ROW_BLOCKS):
-                nc.tensor.transpose(spread[:, q, :], dist[:, q, shift - 1 : shift].to_broadcast([P, P]), ident_f32[:])
-            dist_row = stage.tile([P, COLS], F32)
-            nc.scalar.copy(out=dist_row[:], in_=spread[:].rearrange("p q k -> p (q k)"))
-            return dist_row
+                nc.tensor.transpose(spread[:, q, :], dist[:, shift - 1, q : q + 1].to_broadcast([P, P]), ident_f32[:])
+            nc.scalar.copy(out=dist_rows[:, shift - 1, :], in_=spread[:].rearrange("p q k -> p (q k)"))
+
+        def park_distances():
+            turned = banks.tile([P, P], F32, tag="bank")
+            nc.tensor.transpose(turned[:], dist_square[:], ident_f32[:])
+            dist_t = keep.tile([P, P], F32)
+            nc.scalar.copy(out=dist_t[:], in_=turned[:])
+            parked = out[GRAPHS - 1 : GRAPHS, 0 : DIST_ROWS // NODES, :, :]
+            nc.sync.dma_start(out=parked.rearrange("b i j m -> (b i j) m"), in_=dist_t[0:DIST_ROWS, :])
+            flat = parked.rearrange("b i j m -> (b i j m)")
+            for shift in range(MAX_SHIFT - 1, 0, -1):
+                nc.sync.dma_start(
+                    out=dist_rows[:, shift - 1, :],
+                    in_=flat[(shift - 1) * COLS : shift * COLS].partition_broadcast(P),
+                )
 
         terms = {}
-        rows_of = {}
 
         def start_term(shift):
-            rows_of[shift] = spread_distances(shift)
             next_term = stage.tile([P, F_BLOCKS, COLS], F32, tag="term")
             terms[shift] = next_term
 
-        def distance_term(term, dist_row, j):
+        def distance_term(shift, j):
+            term, dist_row = terms[shift], dist_rows[:, shift - 1, :]
             w_col, b_col = w_dist[:, j : j + 1], bias1[:, j : j + 1]
             if j < SCALAR_BLOCKS:
-                nc.scalar.activation(out=term[:, j, :], in_=dist_row[:], func=ACT.Identity, scale=w_col, bias=b_col)
+                nc.scalar.activation(out=term[:, j, :], in_=dist_row, func=ACT.Identity, scale=w_col, bias=b_col)
             else:
                 nc.gpsimd.tensor_scalar(
-                    out=term[:, j, :], in0=dist_row[:], scalar1=w_col, scalar2=b_col, op0=ALU.mult, op1=ALU.add
+                    out=term[:, j, :], in0=dist_row, scalar1=w_col, scalar2=b_col, op0=ALU.mult, op1=ALU.add
                 )
 
         def node_terms(shift, swapped, c):
@@ -338,21 +356,23 @@ def tile_graphmessagelayer_pa_t_kernel(tc, node_state, positions, We1, be1, We2,
                         last = first + (b1 - b0 - 1) * row_step
                         queue.dma_start(out=out_rows[:, first : last + 1 : row_step, :], in_=result[rows, b0:b1, :])
 
-        def messages(tile):
+        def messages(tile, due):
             msg = msg_banks.tile([P, ROW_BLOCKS, M], F32, tag="msg")
             multiply_w2(msg, *codes[tile], 0, ROW_BLOCKS)
             product = work.tile([P, ROW_BLOCKS, M], F32)
             nc.scalar.copy(out=product[:], in_=msg[:])
-            unfinished.append((product, tile))
+            unfinished.append((due, product, tile))
 
         unfinished = []
 
-        def finish_messages():
-            for product, tile in unfinished:
+        def finish_messages(step):
+            while unfinished and unfinished[0][0] <= step:
+                entry = unfinished[0]
+                unfinished.remove(entry)
+                product, tile = entry[1:3]
                 result = work.tile([P, ROW_BLOCKS, M], F32, bufs=4)
                 nc.gpsimd.tensor_tensor(out=result[:], in0=product[:], in1=be2_all[:], op=ALU.add)
                 store(result, *steps[tile * F_PASSES][0:2], nc.sync)
-            unfinished.clear()
 
         order = [0, *range(MAX_SHIFT, 0, -1)]
         steps = []
@@ -370,6 +390,12 @@ def tile_graphmessagelayer_pa_t_kernel(tc, node_state, positions, We1, be1, We2,
         last_step = len(steps) - 1
         last_tile = last_step // F_PASSES
 
+        quantise_at, multiply_at = {}, {}
+        for tile in range(last_tile):
+            second_half_step = tile * F_PASSES + 1
+            quantise_at[min(second_half_step + QUANTISE_LAG, last_step - last_tile + tile)] = tile
+            if tile < last_tile - 1:
+                multiply_at[min(second_half_step + MESSAGE_LAG, last_step - last_tile + tile + 1)] = tile
         for g in range(len(steps)):
             shift, swapped, c, coming, first_block, share = steps[g]
             tile = g // F_PASSES
@@ -386,9 +412,11 @@ def tile_graphmessagelayer_pa_t_kernel(tc, node_state, positions, We1, be1, We2,
                         quantise_states(coming % COPIES, ahead_cols)
                     start_term(coming)
                 for j in range(first_block, first_block + share):
-                    distance_term(terms[coming], rows_of[coming], j)
+                    distance_term(coming, j)
             pre = work.tile([P, COLS // LINE, PACK, LINE], F32)
             if g == 0:
+                spread_distances(coming)
+                park_distances()
                 start_term(coming)
             accs = node_terms(shift, swapped, c)
             if shift == 0:
@@ -399,7 +427,7 @@ def tile_graphmessagelayer_pa_t_kernel(tc, node_state, positions, We1, be1, We2,
                         for side, engine_copy in ((0, by_vector), (1, by_scalar))
                     ]
                 for j in range(first_block, first_block + share):
-                    distance_term(terms[coming], rows_of[coming], j)
+                    distance_term(coming, j)
                 add_bias(pre, accs, c)
                 apply_silu(hs[tile], pre, c, all_cols)
                 if c == 0:
@@ -416,29 +444,24 @@ def tile_graphmessagelayer_pa_t_kernel(tc, node_state, positions, We1, be1, We2,
                 add_terms(pre, accs, terms[shift], c, all_cols)
                 apply_silu(hs[tile], pre, c, all_cols)
             else:
-                finish_messages()
-                messages(tile - 2)
-                finish_messages()
+                msg = msg_banks.tile([P, ROW_BLOCKS, M], F32, tag="msg")
+                multiply_w2(msg, *codes[tile - 1], 0, ROW_BLOCKS)
                 add_terms(pre, accs, terms[shift], c, halves_of_cols[0])
                 apply_silu(hs[tile], pre, c, halves_of_cols[0])
-                quantise_h(hs[tile - 1], *codes[tile - 1], 0, F_PASSES, all_cols)
+                result = work.tile([P, ROW_BLOCKS, M], F32, bufs=4)
+                nc.vector.tensor_tensor(out=result[:], in0=msg[:], in1=be2_all[:], op=ALU.add)
                 add_terms(pre, accs, terms[shift], c, halves_of_cols[1])
                 apply_silu(hs[tile], pre, c, halves_of_cols[1])
-            ready = g - QUANTISE_LAG
-            if 0 <= ready and steps[ready][2] == F_PASSES - 1:
-                tile = ready // F_PASSES
+                finish_messages(g)
+                store(result, *steps[g - F_PASSES][0:2], nc.sync)
+            if g in quantise_at:
+                tile = quantise_at[g]
                 quantise_h(hs[tile], *codes[tile], 0, F_PASSES, all_cols)
-            finish_messages()
-            done = g - MESSAGE_LAG
-            if 0 <= done and steps[done][2] == F_PASSES - 1:
-                messages(done // F_PASSES)
+            finish_messages(g)
+            if g in multiply_at:
+                messages(multiply_at[g], min(g + ADD_LAG, last_step))
 
-        msg = msg_banks.tile([P, ROW_BLOCKS, M], F32, tag="msg")
-        multiply_w2(msg, *codes[last_tile - 1], 0, ROW_BLOCKS)
         quantise_h(hs[last_tile], *codes[last_tile], 0, 1, all_cols)
-        result = work.tile([P, ROW_BLOCKS, M], F32, bufs=4)
-        nc.vector.tensor_tensor(out=result[:], in0=msg[:], in1=be2_all[:], op=ALU.add)
-        store(result, *steps[last_step - F_PASSES][0:2], nc.sync)
         result = work.tile([P, ROW_BLOCKS, M], F32, bufs=4)
         for half, cols in enumerate(halves_of_cols):
             q0 = half * ROW_BLOCKS // 2

@@ -39,14 +39,14 @@ STATE_COLS = COPY_COLS + (COPIES - 1) * GRAPHS
 REACH = (ROW_BLOCKS - 1) * BLOCK_NODES + MAX_SHIFT + 1
 SMALLEST_SQUARE = 2.0**-100
 
-SCALAR_BLOCKS = 1
+SCALAR_BLOCKS = (3, 4)
 DIST_ROWS = MAX_SHIFT * ROW_BLOCKS
 LINE = 4
 PIECE = K_PASS // 2
 BE2_ROW = 32
 QUANTISE_LAG = 3
-ADD_LAG = 2
-MESSAGE_LAG = 5
+ADD_LAG = 1
+MESSAGE_LAG = 4
 
 FLOPS = 2 * GRAPHS * NODES * H * 2 * F + 2 * GRAPHS * NODES * NODES * F * M
 
@@ -202,6 +202,7 @@ def tile_graphmessagelayer_pa_t_kernel(tc, node_state, positions, We1, be1, We2,
         apart = keep.tile([P, ROW_BLOCKS, MAX_SHIFT], F32)
         nc.vector.tensor_single_scalar(out=apart[:], in_=square[:], scalar=0.0, op=ALU.is_gt)
 
+        g01 = regroup_w1(by_scalar, 0, pieces[1])
         root = keep.tile([P, ROW_BLOCKS, MAX_SHIFT], F32)
         nc.scalar.activation(out=root[:], in_=floored[:], func=ACT.Sqrt)
         nc.scalar.activation(out=warm[:], in_=one[:], func=ACT.Silu)
@@ -210,7 +211,6 @@ def tile_graphmessagelayer_pa_t_kernel(tc, node_state, positions, We1, be1, We2,
         quantise_states(0, own_cols)
         quantise_w1(g00, 0, pieces[0])
         quantise_w1(g10, 1, pieces[0])
-        g01 = regroup_w1(by_vector, 0, pieces[1])
         g11 = regroup_w1(by_vector, 1, pieces[1])
         quantise_w1(g01, 0, pieces[1])
         quantise_w1(g11, 1, pieces[1])
@@ -260,7 +260,7 @@ def tile_graphmessagelayer_pa_t_kernel(tc, node_state, positions, We1, be1, We2,
         def distance_term(shift, j):
             term, dist_row = terms[shift], dist_rows[:, shift - 1, :]
             w_col, b_col = w_dist[:, j : j + 1], bias1[:, j : j + 1]
-            if j < SCALAR_BLOCKS:
+            if j in SCALAR_BLOCKS:
                 nc.scalar.activation(out=term[:, j, :], in_=dist_row, func=ACT.Identity, scale=w_col, bias=b_col)
             else:
                 nc.gpsimd.tensor_scalar(
@@ -405,6 +405,7 @@ def tile_graphmessagelayer_pa_t_kernel(tc, node_state, positions, We1, be1, We2,
                 h_words = work.tile([P, F_PASSES, COLS], U32, align_bytes=64, bufs=4)
                 h_scales = work.tile([P, F_PASSES, COLS], U8, align_bytes=64, bufs=4)
                 codes[tile] = (h_words, h_scales)
+            finish_messages(g)
             if coming > 0 and shift > 0:
                 if first_block == 0:
                     if coming > MAX_SHIFT - COPIES:
@@ -448,16 +449,15 @@ def tile_graphmessagelayer_pa_t_kernel(tc, node_state, positions, We1, be1, We2,
                 multiply_w2(msg, *codes[tile - 1], 0, ROW_BLOCKS)
                 add_terms(pre, accs, terms[shift], c, halves_of_cols[0])
                 apply_silu(hs[tile], pre, c, halves_of_cols[0])
-                result = work.tile([P, ROW_BLOCKS, M], F32, bufs=4)
-                nc.vector.tensor_tensor(out=result[:], in0=msg[:], in1=be2_all[:], op=ALU.add)
                 add_terms(pre, accs, terms[shift], c, halves_of_cols[1])
                 apply_silu(hs[tile], pre, c, halves_of_cols[1])
+                result = work.tile([P, ROW_BLOCKS, M], F32, bufs=4)
+                nc.vector.tensor_tensor(out=result[:], in0=msg[:], in1=be2_all[:], op=ALU.add)
                 finish_messages(g)
                 store(result, *steps[g - F_PASSES][0:2], nc.sync)
             if g in quantise_at:
                 tile = quantise_at[g]
                 quantise_h(hs[tile], *codes[tile], 0, F_PASSES, all_cols)
-            finish_messages(g)
             if g in multiply_at:
                 messages(multiply_at[g], min(g + ADD_LAG, last_step))
 

@@ -7,6 +7,7 @@ F32 = mybir.dt.float32
 BF16 = mybir.dt.bfloat16
 U32 = mybir.dt.uint32
 U8 = mybir.dt.uint8
+I32 = mybir.dt.int32
 FP8X4 = mybir.dt.float8_e4m3fn_x4
 ALU = mybir.AluOpType
 ACT = mybir.ActivationFunctionType
@@ -14,6 +15,7 @@ AXIS = mybir.AxisListType
 
 P = 128
 PACK = 4
+PAIRS = PACK // 2
 K_PASS = P * PACK
 
 GRAPHS = 16
@@ -33,8 +35,7 @@ MAX_SHIFT = NODES // 2
 COPIES = 4
 WINDOW_STEP = COPIES * GRAPHS
 AHEAD_COLS = MAX_SHIFT // COPIES * WINDOW_STEP
-COPY_COLS = COLS + AHEAD_COLS
-STATE_COLS = COPY_COLS + (COPIES - 1) * GRAPHS
+COPY_COLS = COLS + AHEAD_COLS + WINDOW_STEP
 
 REACH = (ROW_BLOCKS - 1) * BLOCK_NODES + MAX_SHIFT + 1
 SMALLEST_SQUARE = 2.0**-100
@@ -68,12 +69,12 @@ def tile_graphmessagelayer_pa_t_kernel(tc, node_state, positions, We1, be1, We2,
         msg_banks = ctx.enter_context(tc.psum_pool(name="msg_banks", bufs=2))
         ctx.enter_context(tc.manual_schedule())
 
-        vectors = keep.tile([P, P], BF16)
-        nc.vector.memset(vectors[:], 0.0)
         pos_rows = keep.tile([P, 2, NODES * COORDS], BF16)
         nc.vector.memset(pos_rows[:], 0.0)
         for copy in range(2):
-            nc.scalar.dma_start(out=pos_rows[0:GRAPHS, copy, :], in_=positions.rearrange("b u c -> b (u c)"))
+            nc.sync.dma_start(out=pos_rows[0:GRAPHS, copy, :], in_=positions.rearrange("b u c -> b (u c)"))
+        vectors = keep.tile([P, P], BF16)
+        nc.vector.memset(vectors[:], 0.0)
         nc.scalar.dma_start(
             out=vectors[0:F_BLOCKS, :], in_=We1[2 * H : 2 * H + 1, :].rearrange("o (j p) -> (o j) p", p=P)
         )
@@ -81,14 +82,16 @@ def tile_graphmessagelayer_pa_t_kernel(tc, node_state, positions, We1, be1, We2,
         nc.scalar.dma_start(out=vectors[BE2_ROW : BE2_ROW + 1, :], in_=be2.unsqueeze(0))
 
         x_rows = keep.tile([P, GRAPHS // 4, H], BF16)
-        nc.sync.dma_start(out=x_rows[:], in_=node_state.rearrange("(g bl) u k -> (bl u) g k", bl=4))
+        x_view = node_state.rearrange("(g bl) u k -> (bl u) g k", bl=4)
+        for g in (0, 2):
+            nc.sync.dma_start(out=x_rows[:, g : g + 2, :], in_=x_view[:, g : g + 2, :])
         w1_rows = keep.tile([P, 2 * PACK, F], BF16)
-        w1_view = We1[0 : 2 * H, :].rearrange("(j p) f -> p j f", p=P)
+        w1_view = [We1[side * H : (side + 1) * H, :].rearrange("(p t) f -> p t f", t=PACK) for side in range(2)]
         for c in range(F_PASSES):
             f_half = slice(c * K_PASS, (c + 1) * K_PASS)
             for side in range(2):
                 blocks = slice(side * PACK, (side + 1) * PACK)
-                nc.sync.dma_start(out=w1_rows[:, blocks, f_half], in_=w1_view[:, blocks, f_half])
+                nc.sync.dma_start(out=w1_rows[:, blocks, f_half], in_=w1_view[side][:, :, f_half])
         w2_rows = keep.tile([P, F_BLOCKS, M], BF16)
         nc.sync.dma_start(out=w2_rows[:], in_=We2.rearrange("(j p) m -> p j m", p=P))
 
@@ -102,68 +105,48 @@ def tile_graphmessagelayer_pa_t_kernel(tc, node_state, positions, We1, be1, We2,
         ident_bf16 = wide[:, left : left + P]
         ident_f32 = keep.tile([P, P], F32)
         make_identity(nc, ident_f32[:])
+        x_words = keep.tile([P, COPIES, COPY_COLS], U32, align_bytes=64)
+        x_scales = keep.tile([P, COPIES, COPY_COLS], U8, align_bytes=64)
+        nc.gpsimd.memset(x_scales[:].rearrange("p c w -> p (c w)").bitcast(I32), 0)
         one = keep.tile([P, 1], F32)
         nc.vector.memset(one[:], 1.0)
         warm = keep.tile([P, 1], F32)
         nc.scalar.activation(out=warm[:], in_=one[:], func=ACT.Sqrt)
 
-        states = keep.tile([P, STATE_COLS, PACK], BF16, align_bytes=64)
-        by_node = states[:, 0:COLS, :].rearrange("p (u b) t -> p u b t", b=GRAPHS)
+        states = keep.tile([P, COLS, PACK], BF16, align_bytes=64)
+        by_node = states[:].rearrange("p w t -> p (w t)").bitcast(F32).rearrange(
+            "p (u b r) -> p u b r", b=GRAPHS, r=PAIRS
+        )
 
         def turn_states(engine_copy, g):
-            x_t = banks.tile([P, PACK, P], BF16, tag="bank")
-            for t in range(PACK):
-                nc.tensor.transpose(x_t[:, t, :], x_rows[:, g, t * P : (t + 1) * P], ident_bf16)
+            x_t = banks.tile([P, PAIRS, P], F32, tag="bank")
+            x_pairs = x_rows[:, g, :].bitcast(F32)
+            for r in range(PAIRS):
+                nc.tensor.transpose(x_t[:, r, :], x_pairs[:, r : H // 2 : PAIRS], ident_f32[:])
             engine_copy(
-                out=by_node[:, :, 4 * g : 4 * g + 4, :], in_=x_t[:].rearrange("p t (bl u) -> p u bl t", u=NODES)
+                out=by_node[:, :, 4 * g : 4 * g + 4, :], in_=x_t[:].rearrange("p r (bl u) -> p u bl r", u=NODES)
             )
 
         by_vector = nc.vector.tensor_copy
         by_scalar = nc.scalar.copy
-        turn_states(by_vector, 0)
-        turn_states(by_scalar, 1)
-        turn_states(by_vector, 2)
-        x_words = keep.tile([P, COPIES, COPY_COLS], U32, align_bytes=64)
-        x_scales = keep.tile([P, COPIES, COPY_COLS], U8, align_bytes=64)
-
-        def quantise_states(copy, cols):
-            first = copy * GRAPHS
+        def quantise_states():
             nc.vector.quantize_mx(
-                out=x_words[:, copy, cols].bitcast(FP8X4),
-                scales=x_scales[:, copy, cols],
-                in_=states[:, first + cols.start : first + cols.stop, :].rearrange("p w t -> p (w t)"),
+                out=x_words[:, 0, 0:COLS].bitcast(FP8X4),
+                scales=x_scales[:, 0, 0:COLS],
+                in_=states[:].rearrange("p w t -> p (w t)"),
             )
 
-        own_cols = slice(0, COLS)
-        ahead_cols = slice(COLS, COPY_COLS)
+        def move_states(to_copy, first_col, from_col, n_cols):
+            for rows in (x_words, x_scales):
+                nc.sync.dma_start(
+                    out=rows[:, to_copy, first_col : first_col + n_cols].bitcast(I32),
+                    in_=rows[:, 0, from_col : from_col + n_cols].bitcast(I32),
+                )
 
-        around_bank = banks.tile([P, REACH, COORDS], F32, tag="bank")
-        pos_round = pos_rows[:].rearrange("p r x -> p (r x)")
-        for lane in range(BLOCK_NODES):
-            nc.tensor.matmul(
-                around_bank[:].rearrange("p n x -> p (n x)"),
-                lhsT=wide[:, left - lane * GRAPHS : left - lane * GRAPHS + P],
-                rhs=pos_round[:, lane * COORDS : (lane + REACH) * COORDS],
-                start=(lane == 0),
-                stop=(lane == BLOCK_NODES - 1),
-            )
-        around = keep.tile([P, REACH, COORDS], F32)
-        nc.scalar.copy(out=around[:], in_=around_bank[:])
-        turn_states(by_scalar, 3)
-        vectors_t = banks.tile([P, P], BF16, tag="bank")
-        nc.tensor.transpose(vectors_t[:], vectors[:], ident_bf16)
-        be2_bank = msg_banks.tile([P, M], F32, tag="msg")
-        nc.tensor.matmul(
-            be2_bank[:],
-            lhsT=ident_bf16[:, BE2_ROW : BE2_ROW + 1].to_broadcast([P, P]),
-            rhs=vectors[:],
-            start=True,
-            stop=True,
-        )
-        per_feature = keep.tile([P, 2 * F_BLOCKS], F32)
-        nc.scalar.copy(out=per_feature[:], in_=vectors_t[:, 0 : 2 * F_BLOCKS])
-        w_dist = per_feature[:, 0:F_BLOCKS]
-        bias1 = per_feature[:, F_BLOCKS : 2 * F_BLOCKS]
+        def copy_states():
+            move_states(0, COLS, 0, COPY_COLS - COLS)
+            for copy in range(1, COPIES):
+                move_states(copy, 0, copy * GRAPHS, COLS + AHEAD_COLS)
 
         w1_words = keep.tile([P, 2, F], U32, align_bytes=64)
         w1_scales = keep.tile([P, 2, F], U8, align_bytes=64)
@@ -181,10 +164,31 @@ def tile_graphmessagelayer_pa_t_kernel(tc, node_state, positions, We1, be1, We2,
             )
 
         pieces = [slice(k * PIECE, (k + 1) * PIECE) for k in range(F // PIECE)]
-        g00 = regroup_w1(by_vector, 0, pieces[0])
 
         dist = dist_square[:, 0:DIST_ROWS].rearrange("p (s q) -> p s q", q=ROW_BLOCKS)
         delta = keep.tile([P, ROW_BLOCKS, MAX_SHIFT, COORDS], F32)
+        delta_sq = keep.tile([P, ROW_BLOCKS, MAX_SHIFT, COORDS], F32)
+        square = keep.tile([P, ROW_BLOCKS, MAX_SHIFT], F32)
+        floored = keep.tile([P, ROW_BLOCKS, MAX_SHIFT], F32)
+        apart = keep.tile([P, ROW_BLOCKS, MAX_SHIFT], F32)
+        root = keep.tile([P, ROW_BLOCKS, MAX_SHIFT], F32)
+
+        turn_states(by_vector, 0)
+        turn_states(by_scalar, 1)
+        turn_states(by_vector, 2)
+        turn_states(by_scalar, 3)
+        around_bank = msg_banks.tile([P, REACH, COORDS], F32, tag="msg")
+        pos_round = pos_rows[:].rearrange("p r x -> p (r x)")
+        for lane in range(BLOCK_NODES):
+            nc.tensor.matmul(
+                around_bank[:].rearrange("p n x -> p (n x)"),
+                lhsT=wide[:, left - lane * GRAPHS : left - lane * GRAPHS + P],
+                rhs=pos_round[:, lane * COORDS : (lane + REACH) * COORDS],
+                start=(lane == 0),
+                stop=(lane == BLOCK_NODES - 1),
+            )
+        around = keep.tile([P, REACH, COORDS], F32)
+        nc.scalar.copy(out=around[:], in_=around_bank[:])
         for q in range(ROW_BLOCKS):
             first = q * BLOCK_NODES
             nc.vector.tensor_tensor(
@@ -193,26 +197,22 @@ def tile_graphmessagelayer_pa_t_kernel(tc, node_state, positions, We1, be1, We2,
                 in1=around[:, first : first + 1, :].to_broadcast([P, MAX_SHIFT, COORDS]),
                 op=ALU.subtract,
             )
-        delta_sq = keep.tile([P, ROW_BLOCKS, MAX_SHIFT, COORDS], F32)
+        g00 = regroup_w1(by_vector, 0, pieces[0])
         nc.vector.tensor_tensor(out=delta_sq[:], in0=delta[:], in1=delta[:], op=ALU.mult)
-        square = keep.tile([P, ROW_BLOCKS, MAX_SHIFT], F32)
+        quantise_states()
+        copy_states()
         nc.vector.tensor_reduce(out=square[:], in_=delta_sq[:], axis=AXIS.X, op=ALU.add)
-        floored = keep.tile([P, ROW_BLOCKS, MAX_SHIFT], F32)
-        nc.vector.tensor_scalar_max(out=floored[:], in0=square[:], scalar1=SMALLEST_SQUARE)
-        apart = keep.tile([P, ROW_BLOCKS, MAX_SHIFT], F32)
-        nc.vector.tensor_single_scalar(out=apart[:], in_=square[:], scalar=0.0, op=ALU.is_gt)
-
         g01 = regroup_w1(by_scalar, 0, pieces[1])
-        root = keep.tile([P, ROW_BLOCKS, MAX_SHIFT], F32)
+        quantise_w1(g00, 0, pieces[0])
+        nc.vector.tensor_scalar_max(out=floored[:], in0=square[:], scalar1=SMALLEST_SQUARE)
+        nc.vector.tensor_single_scalar(out=apart[:], in_=square[:], scalar=0.0, op=ALU.is_gt)
         nc.scalar.activation(out=root[:], in_=floored[:], func=ACT.Sqrt)
         nc.scalar.activation(out=warm[:], in_=one[:], func=ACT.Silu)
         g10 = regroup_w1(by_vector, 1, pieces[0])
-        nc.vector.tensor_tensor(out=dist.rearrange("p s q -> p q s"), in0=root[:], in1=apart[:], op=ALU.mult)
-        quantise_states(0, own_cols)
-        quantise_w1(g00, 0, pieces[0])
+        quantise_w1(g01, 0, pieces[1])
         quantise_w1(g10, 1, pieces[0])
         g11 = regroup_w1(by_vector, 1, pieces[1])
-        quantise_w1(g01, 0, pieces[1])
+        nc.vector.tensor_tensor(out=dist.rearrange("p s q -> p q s"), in0=root[:], in1=apart[:], op=ALU.mult)
         quantise_w1(g11, 1, pieces[1])
 
         be2_all = keep.tile([P, ROW_BLOCKS, M], F32)
@@ -232,13 +232,13 @@ def tile_graphmessagelayer_pa_t_kernel(tc, node_state, positions, We1, be1, We2,
         dist_rows = keep.tile([P, MAX_SHIFT, COLS], F32)
 
         def spread_distances(shift):
-            spread = banks.tile([P, ROW_BLOCKS, P], F32, tag="bank")
+            spread = msg_banks.tile([P, ROW_BLOCKS, P], F32, tag="msg")
             for q in range(ROW_BLOCKS):
                 nc.tensor.transpose(spread[:, q, :], dist[:, shift - 1, q : q + 1].to_broadcast([P, P]), ident_f32[:])
             nc.scalar.copy(out=dist_rows[:, shift - 1, :], in_=spread[:].rearrange("p q k -> p (q k)"))
 
         def park_distances():
-            turned = banks.tile([P, P], F32, tag="bank")
+            turned = msg_banks.tile([P, P], F32, tag="msg")
             nc.tensor.transpose(turned[:], dist_square[:], ident_f32[:])
             dist_t = keep.tile([P, P], F32)
             nc.scalar.copy(out=dist_t[:], in_=turned[:])
@@ -251,6 +251,9 @@ def tile_graphmessagelayer_pa_t_kernel(tc, node_state, positions, We1, be1, We2,
                     in_=flat[(shift - 1) * COLS : shift * COLS].partition_broadcast(P),
                 )
 
+        per_feature = keep.tile([P, 2 * F_BLOCKS], F32)
+        w_dist = per_feature[:, 0:F_BLOCKS]
+        bias1 = per_feature[:, F_BLOCKS : 2 * F_BLOCKS]
         terms = {}
 
         def start_term(shift):
@@ -260,7 +263,7 @@ def tile_graphmessagelayer_pa_t_kernel(tc, node_state, positions, We1, be1, We2,
         def distance_term(shift, j):
             term, dist_row = terms[shift], dist_rows[:, shift - 1, :]
             w_col, b_col = w_dist[:, j : j + 1], bias1[:, j : j + 1]
-            if j in SCALAR_BLOCKS:
+            if j in SCALAR_BLOCKS and shift < MAX_SHIFT:
                 nc.scalar.activation(out=term[:, j, :], in_=dist_row, func=ACT.Identity, scale=w_col, bias=b_col)
             else:
                 nc.gpsimd.tensor_scalar(
@@ -396,7 +399,45 @@ def tile_graphmessagelayer_pa_t_kernel(tc, node_state, positions, We1, be1, We2,
             quantise_at[min(second_half_step + QUANTISE_LAG, last_step - last_tile + tile)] = tile
             if tile < last_tile - 1:
                 multiply_at[min(second_half_step + MESSAGE_LAG, last_step - last_tile + tile + 1)] = tile
-        for g in range(len(steps)):
+        h = work.tile([P, F_PASSES, COLS, PACK], BF16, align_bytes=64)
+        hs[0] = h
+        h_words = work.tile([P, F_PASSES, COLS], U32, align_bytes=64, bufs=4)
+        h_scales = work.tile([P, F_PASSES, COLS], U8, align_bytes=64, bufs=4)
+        codes[0] = (h_words, h_scales)
+        accs0 = node_terms(0, False, 0)
+        vectors_t = msg_banks.tile([P, P], BF16, tag="msg")
+        nc.tensor.transpose(vectors_t[:], vectors[:], ident_bf16)
+        second_half = []
+        for cols in pieces[2:4]:
+            for side, engine_copy in ((0, by_vector), (1, by_scalar)):
+                second_half.append((regroup_w1(engine_copy, side, cols), side, cols))
+        nc.scalar.copy(out=per_feature[:], in_=vectors_t[:, 0 : 2 * F_BLOCKS])
+        spread_distances(MAX_SHIFT)
+        for piece in second_half:
+            quantise_w1(*piece)
+        prepare_w2()
+        park_distances()
+        pre0 = work.tile([P, COLS // LINE, PACK, LINE], F32, tag="pre")
+        add_bias(pre0, accs0, 0)
+        accs1 = node_terms(0, False, 1)
+        start_term(MAX_SHIFT)
+        for j in range(F_BLOCKS):
+            distance_term(MAX_SHIFT, j)
+        pre1 = work.tile([P, COLS // LINE, PACK, LINE], F32, tag="pre")
+        add_bias(pre1, accs1, 1)
+        apply_silu(hs[0], pre0, 0, all_cols)
+        apply_silu(hs[0], pre1, 1, all_cols)
+        be2_bank = msg_banks.tile([P, M], F32, tag="msg")
+        nc.tensor.matmul(
+            be2_bank[:],
+            lhsT=ident_bf16[:, BE2_ROW : BE2_ROW + 1].to_broadcast([P, P]),
+            rhs=vectors[:],
+            start=True,
+            stop=True,
+        )
+        nc.scalar.copy(out=be2_all[:], in_=be2_bank[:].unsqueeze(1).to_broadcast([P, ROW_BLOCKS, M]))
+
+        for g in range(F_PASSES, len(steps)):
             shift, swapped, c, coming, first_block, share = steps[g]
             tile = g // F_PASSES
             if c == 0:
@@ -406,42 +447,14 @@ def tile_graphmessagelayer_pa_t_kernel(tc, node_state, positions, We1, be1, We2,
                 h_scales = work.tile([P, F_PASSES, COLS], U8, align_bytes=64, bufs=4)
                 codes[tile] = (h_words, h_scales)
             finish_messages(g)
-            if coming > 0 and shift > 0:
+            if coming > 0:
                 if first_block == 0:
-                    if coming > MAX_SHIFT - COPIES:
-                        quantise_states(coming % COPIES, own_cols)
-                        quantise_states(coming % COPIES, ahead_cols)
                     start_term(coming)
                 for j in range(first_block, first_block + share):
                     distance_term(coming, j)
-            pre = work.tile([P, COLS // LINE, PACK, LINE], F32)
-            if g == 0:
-                spread_distances(coming)
-                park_distances()
-                start_term(coming)
+            pre = work.tile([P, COLS // LINE, PACK, LINE], F32, tag="pre")
             accs = node_terms(shift, swapped, c)
-            if shift == 0:
-                if c == 0:
-                    second_half = [
-                        (regroup_w1(engine_copy, side, cols), side, cols)
-                        for cols in pieces[2:4]
-                        for side, engine_copy in ((0, by_vector), (1, by_scalar))
-                    ]
-                for j in range(first_block, first_block + share):
-                    distance_term(coming, j)
-                add_bias(pre, accs, c)
-                apply_silu(hs[tile], pre, c, all_cols)
-                if c == 0:
-                    for piece in second_half:
-                        quantise_w1(*piece)
-                    nc.vector.tensor_copy(
-                        out=states[:, COLS:STATE_COLS, :], in_=states[:, 0 : STATE_COLS - COLS, :]
-                    )
-                    quantise_states(0, ahead_cols)
-                else:
-                    prepare_w2()
-                    nc.scalar.copy(out=be2_all[:], in_=be2_bank[:].unsqueeze(1).to_broadcast([P, ROW_BLOCKS, M]))
-            elif g < last_step:
+            if g < last_step:
                 add_terms(pre, accs, terms[shift], c, all_cols)
                 apply_silu(hs[tile], pre, c, all_cols)
             else:

@@ -35,7 +35,7 @@ MAX_SHIFT = NODES // 2
 COPIES = 4
 WINDOW_STEP = COPIES * GRAPHS
 AHEAD_COLS = MAX_SHIFT // COPIES * WINDOW_STEP
-COPY_COLS = COLS + AHEAD_COLS + WINDOW_STEP
+COPY_COLS = COLS + AHEAD_COLS + 256
 
 REACH = (ROW_BLOCKS - 1) * BLOCK_NODES + MAX_SHIFT + 1
 SMALLEST_SQUARE = 2.0**-100
@@ -105,15 +105,15 @@ def tile_graphmessagelayer_pa_t_kernel(tc, node_state, positions, We1, be1, We2,
         ident_bf16 = wide[:, left : left + P]
         ident_f32 = keep.tile([P, P], F32)
         make_identity(nc, ident_f32[:])
-        x_words = keep.tile([P, COPIES, COPY_COLS], U32, align_bytes=64)
-        x_scales = keep.tile([P, COPIES, COPY_COLS], U8, align_bytes=64)
+        x_words = keep.tile([P, COPIES, COPY_COLS], U32, align_bytes=256)
+        x_scales = keep.tile([P, COPIES, COPY_COLS], U8, align_bytes=256)
         nc.gpsimd.memset(x_scales[:].rearrange("p c w -> p (c w)").bitcast(I32), 0)
         one = keep.tile([P, 1], F32)
         nc.vector.memset(one[:], 1.0)
         warm = keep.tile([P, 1], F32)
         nc.scalar.activation(out=warm[:], in_=one[:], func=ACT.Sqrt)
 
-        states = keep.tile([P, COLS, PACK], BF16, align_bytes=64)
+        states = keep.tile([P, COLS, PACK], BF16, align_bytes=256)
         by_node = states[:].rearrange("p w t -> p (w t)").bitcast(F32).rearrange(
             "p (u b r) -> p u b r", b=GRAPHS, r=PAIRS
         )
@@ -148,8 +148,8 @@ def tile_graphmessagelayer_pa_t_kernel(tc, node_state, positions, We1, be1, We2,
             for copy in range(1, COPIES):
                 move_states(copy, 0, copy * GRAPHS, COLS + AHEAD_COLS)
 
-        w1_words = keep.tile([P, 2, F], U32, align_bytes=64)
-        w1_scales = keep.tile([P, 2, F], U8, align_bytes=64)
+        w1_words = keep.tile([P, 2, F], U32, align_bytes=256)
+        w1_scales = keep.tile([P, 2, F], U8, align_bytes=256)
 
         def regroup_w1(engine_copy, side, cols):
             grouped = stage.tile([P, PIECE, PACK], BF16, align_bytes=64, bufs=8, tag="w1_grouped")
@@ -216,9 +216,9 @@ def tile_graphmessagelayer_pa_t_kernel(tc, node_state, positions, We1, be1, We2,
         quantise_w1(g11, 1, pieces[1])
 
         be2_all = keep.tile([P, ROW_BLOCKS, M], F32)
-        w2_grouped = keep.tile([P, F_PASSES, M, PACK], BF16, align_bytes=64)
-        w2_words = keep.tile([P, F_PASSES * M], U32, align_bytes=64)
-        w2_scales = keep.tile([P, F_PASSES * M], U8, align_bytes=64)
+        w2_grouped = keep.tile([P, F_PASSES, M, PACK], BF16, align_bytes=256)
+        w2_words = keep.tile([P, F_PASSES * M], U32, align_bytes=256)
+        w2_scales = keep.tile([P, F_PASSES * M], U8, align_bytes=256)
 
         def prepare_w2():
             for c in range(F_PASSES):
@@ -399,10 +399,10 @@ def tile_graphmessagelayer_pa_t_kernel(tc, node_state, positions, We1, be1, We2,
             quantise_at[min(second_half_step + QUANTISE_LAG, last_step - last_tile + tile)] = tile
             if tile < last_tile - 1:
                 multiply_at[min(second_half_step + MESSAGE_LAG, last_step - last_tile + tile + 1)] = tile
-        h = work.tile([P, F_PASSES, COLS, PACK], BF16, align_bytes=64)
+        h = work.tile([P, F_PASSES, COLS, PACK], BF16, align_bytes=256)
         hs[0] = h
-        h_words = work.tile([P, F_PASSES, COLS], U32, align_bytes=64, bufs=4)
-        h_scales = work.tile([P, F_PASSES, COLS], U8, align_bytes=64, bufs=4)
+        h_words = work.tile([P, F_PASSES, COLS], U32, align_bytes=256, bufs=4)
+        h_scales = work.tile([P, F_PASSES, COLS], U8, align_bytes=256, bufs=4)
         codes[0] = (h_words, h_scales)
         accs0 = node_terms(0, False, 0)
         vectors_t = msg_banks.tile([P, P], BF16, tag="msg")
@@ -441,10 +441,10 @@ def tile_graphmessagelayer_pa_t_kernel(tc, node_state, positions, We1, be1, We2,
             shift, swapped, c, coming, first_block, share = steps[g]
             tile = g // F_PASSES
             if c == 0:
-                h = work.tile([P, F_PASSES, COLS, PACK], BF16, align_bytes=64)
+                h = work.tile([P, F_PASSES, COLS, PACK], BF16, align_bytes=256)
                 hs[tile] = h
-                h_words = work.tile([P, F_PASSES, COLS], U32, align_bytes=64, bufs=4)
-                h_scales = work.tile([P, F_PASSES, COLS], U8, align_bytes=64, bufs=4)
+                h_words = work.tile([P, F_PASSES, COLS], U32, align_bytes=256, bufs=4)
+                h_scales = work.tile([P, F_PASSES, COLS], U8, align_bytes=256, bufs=4)
                 codes[tile] = (h_words, h_scales)
             finish_messages(g)
             if coming > 0:

@@ -85,7 +85,8 @@ def tile_graphmessagelayer_pa_t_kernel(tc, node_state, positions, We1, be1, We2,
         x_view = node_state.rearrange("(g bl) u k -> (bl u) g k", bl=4)
         for g in (0, 2):
             nc.sync.dma_start(out=x_rows[:, g : g + 2, :], in_=x_view[:, g : g + 2, :])
-        w1_rows = keep.tile([P, 2 * PACK, F], BF16)
+        w1_space = stage.tile([P, 4 * PACK * F], BF16, align_bytes=64, tag="term")
+        w1_rows = w1_space[:, 0 : 2 * PACK * F].rearrange("p (j f) -> p j f", f=F)
         w1_view = [We1[side * H : (side + 1) * H, :].rearrange("(p t) f -> p t f", t=PACK) for side in range(2)]
         for c in range(F_PASSES):
             f_half = slice(c * K_PASS, (c + 1) * K_PASS)
@@ -152,15 +153,20 @@ def tile_graphmessagelayer_pa_t_kernel(tc, node_state, positions, We1, be1, We2,
         w1_scales = keep.tile([P, 2, F], U8, align_bytes=256)
 
         def regroup_w1(engine_copy, side, cols):
-            grouped = stage.tile([P, PIECE, PACK], BF16, align_bytes=64, bufs=8, tag="w1_grouped")
-            regroup(engine_copy, grouped[:], w1_rows[:, side * PACK : (side + 1) * PACK, cols])
+            first = 2 * PACK * F + (side * F + cols.start) * PACK
+            grouped = w1_space[:, first : first + PIECE * PACK]
+            regroup(
+                engine_copy,
+                grouped.rearrange("p (w t) -> p w t", t=PACK),
+                w1_rows[:, side * PACK : (side + 1) * PACK, cols],
+            )
             return grouped
 
         def quantise_w1(grouped, side, cols):
             nc.vector.quantize_mx(
                 out=w1_words[:, side, cols].bitcast(FP8X4),
                 scales=w1_scales[:, side, cols],
-                in_=grouped[:].rearrange("p w t -> p (w t)"),
+                in_=grouped,
             )
 
         pieces = [slice(k * PIECE, (k + 1) * PIECE) for k in range(F // PIECE)]
@@ -256,18 +262,21 @@ def tile_graphmessagelayer_pa_t_kernel(tc, node_state, positions, We1, be1, We2,
         bias1 = per_feature[:, F_BLOCKS : 2 * F_BLOCKS]
         terms = {}
 
-        def start_term(shift):
-            next_term = stage.tile([P, F_BLOCKS, COLS], F32, tag="term")
-            terms[shift] = next_term
+        def start_terms(group):
+            room = stage.tile([P, F_BLOCKS, len(group), COLS], F32, align_bytes=64, tag="term")
+            for k, shift in enumerate(reversed(group)):
+                terms[shift] = room[:, :, k, :]
+            terms[group] = room
 
-        def distance_term(shift, j):
-            term, dist_row = terms[shift], dist_rows[:, shift - 1, :]
+        def distance_term(group, j, on_scalar):
+            term = terms[group][:, j].rearrange("p s e -> p (s e)")
+            dist_row = dist_rows[:, group[-1] - 1 : group[0], :].rearrange("p s e -> p (s e)")
             w_col, b_col = w_dist[:, j : j + 1], bias1[:, j : j + 1]
-            if j in SCALAR_BLOCKS and shift < MAX_SHIFT:
-                nc.scalar.activation(out=term[:, j, :], in_=dist_row, func=ACT.Identity, scale=w_col, bias=b_col)
+            if on_scalar:
+                nc.scalar.activation(out=term, in_=dist_row, func=ACT.Identity, scale=w_col, bias=b_col)
             else:
                 nc.gpsimd.tensor_scalar(
-                    out=term[:, j, :], in0=dist_row, scalar1=w_col, scalar2=b_col, op0=ALU.mult, op1=ALU.add
+                    out=term, in0=dist_row, scalar1=w_col, scalar2=b_col, op0=ALU.mult, op1=ALU.add
                 )
 
         def node_terms(shift, swapped, c):
@@ -377,15 +386,20 @@ def tile_graphmessagelayer_pa_t_kernel(tc, node_state, positions, We1, be1, We2,
                 nc.gpsimd.tensor_tensor(out=result[:], in0=product[:], in1=be2_all[:], op=ALU.add)
                 store(result, *steps[tile * F_PASSES][0:2], nc.sync)
 
-        order = [0, *range(MAX_SHIFT, 0, -1)]
+        groups = [(0,), (MAX_SHIFT,), (MAX_SHIFT - 1,), *((s, s - 1) for s in range(MAX_SHIFT - 2, 0, -2))]
         steps = []
-        for shift, coming in zip(order, (*order[1:], 0)):
-            directions = (False, True) if 0 < shift < MAX_SHIFT else (False,)
-            halves = [(swapped, c) for swapped in directions for c in range(F_PASSES)]
+        for group, coming in zip(groups, (*groups[1:], ())):
+            halves = [
+                (shift, swapped, c)
+                for shift in group
+                for swapped in ((False, True) if 0 < shift < MAX_SHIFT else (False,))
+                for c in range(F_PASSES)
+            ]
             share = F_BLOCKS // len(halves)
-            for k, (swapped, c) in enumerate(halves):
-                steps.append((shift, swapped, c, coming, k * share, share))
+            for k, half in enumerate(halves):
+                steps.append((*half, coming, range(k * share, (k + 1) * share)))
 
+        scalar_blocks = {groups[2]: SCALAR_BLOCKS, groups[3]: (3, 6)}
         all_cols = slice(0, COLS)
         halves_of_cols = (slice(0, COLS // 2), slice(COLS // 2, COLS))
         hs = {}
@@ -420,9 +434,9 @@ def tile_graphmessagelayer_pa_t_kernel(tc, node_state, positions, We1, be1, We2,
         pre0 = work.tile([P, COLS // LINE, PACK, LINE], F32, tag="pre")
         add_bias(pre0, accs0, 0)
         accs1 = node_terms(0, False, 1)
-        start_term(MAX_SHIFT)
+        start_terms((MAX_SHIFT,))
         for j in range(F_BLOCKS):
-            distance_term(MAX_SHIFT, j)
+            distance_term((MAX_SHIFT,), j, False)
         pre1 = work.tile([P, COLS // LINE, PACK, LINE], F32, tag="pre")
         add_bias(pre1, accs1, 1)
         apply_silu(hs[0], pre0, 0, all_cols)
@@ -438,7 +452,7 @@ def tile_graphmessagelayer_pa_t_kernel(tc, node_state, positions, We1, be1, We2,
         nc.scalar.copy(out=be2_all[:], in_=be2_bank[:].unsqueeze(1).to_broadcast([P, ROW_BLOCKS, M]))
 
         for g in range(F_PASSES, len(steps)):
-            shift, swapped, c, coming, first_block, share = steps[g]
+            shift, swapped, c, coming, blocks = steps[g]
             tile = g // F_PASSES
             if c == 0:
                 h = work.tile([P, F_PASSES, COLS, PACK], BF16, align_bytes=256)
@@ -447,11 +461,11 @@ def tile_graphmessagelayer_pa_t_kernel(tc, node_state, positions, We1, be1, We2,
                 h_scales = work.tile([P, F_PASSES, COLS], U8, align_bytes=256, bufs=4)
                 codes[tile] = (h_words, h_scales)
             finish_messages(g)
-            if coming > 0:
-                if first_block == 0:
-                    start_term(coming)
-                for j in range(first_block, first_block + share):
-                    distance_term(coming, j)
+            if coming:
+                if 0 in blocks:
+                    start_terms(coming)
+                for j in blocks:
+                    distance_term(coming, j, j in scalar_blocks.get(coming, ()))
             pre = work.tile([P, COLS // LINE, PACK, LINE], F32, tag="pre")
             accs = node_terms(shift, swapped, c)
             if g < last_step:

@@ -32,15 +32,17 @@ ROW_BLOCKS = COLS // P
 BLOCK_NODES = P // GRAPHS
 MAX_SHIFT = NODES // 2
 
+HALF_COLS = COLS // 2
 COPIES = 4
 WINDOW_STEP = COPIES * GRAPHS
 AHEAD_COLS = MAX_SHIFT // COPIES * WINDOW_STEP
-COPY_COLS = COLS + AHEAD_COLS + 256
+COPY_COLS = COLS + AHEAD_COLS + WINDOW_STEP
 
 REACH = (ROW_BLOCKS - 1) * BLOCK_NODES + MAX_SHIFT + 1
 SMALLEST_SQUARE = 2.0**-100
 
 SCALAR_BLOCKS = (3, 4)
+ZERO = -1
 DIST_ROWS = MAX_SHIFT * ROW_BLOCKS
 LINE = 4
 PIECE = K_PASS // 2
@@ -71,8 +73,6 @@ def tile_graphmessagelayer_pa_t_kernel(tc, node_state, positions, We1, be1, We2,
 
         pos_rows = keep.tile([P, 2, NODES * COORDS], BF16)
         nc.vector.memset(pos_rows[:], 0.0)
-        for copy in range(2):
-            nc.sync.dma_start(out=pos_rows[0:GRAPHS, copy, :], in_=positions.rearrange("b u c -> b (u c)"))
         vectors = keep.tile([P, P], BF16)
         nc.vector.memset(vectors[:], 0.0)
         nc.scalar.dma_start(
@@ -81,10 +81,13 @@ def tile_graphmessagelayer_pa_t_kernel(tc, node_state, positions, We1, be1, We2,
         nc.scalar.dma_start(out=vectors[F_BLOCKS : 2 * F_BLOCKS, :], in_=be1.rearrange("(j p) -> j p", p=P))
         nc.scalar.dma_start(out=vectors[BE2_ROW : BE2_ROW + 1, :], in_=be2.unsqueeze(0))
 
-        x_rows = keep.tile([P, GRAPHS // 4, H], BF16)
+        early = keep.tile([P, 2 * PACK * COLS], BF16, align_bytes=256)
+        x_rows = early[:, 0 : PACK * COLS].rearrange("p (g k) -> p g k", k=H)
         x_view = node_state.rearrange("(g bl) u k -> (bl u) g k", bl=4)
         for g in (0, 2):
             nc.sync.dma_start(out=x_rows[:, g : g + 2, :], in_=x_view[:, g : g + 2, :])
+        for copy in range(2):
+            nc.sync.dma_start(out=pos_rows[0:GRAPHS, copy, :], in_=positions.rearrange("b u c -> b (u c)"))
         w1_space = stage.tile([P, 4 * PACK * F], BF16, align_bytes=64, tag="term")
         w1_rows = w1_space[:, 0 : 2 * PACK * F].rearrange("p (j f) -> p j f", f=F)
         w1_view = [We1[side * H : (side + 1) * H, :].rearrange("(p t) f -> p t f", t=PACK) for side in range(2)]
@@ -114,8 +117,8 @@ def tile_graphmessagelayer_pa_t_kernel(tc, node_state, positions, We1, be1, We2,
         warm = keep.tile([P, 1], F32)
         nc.scalar.activation(out=warm[:], in_=one[:], func=ACT.Sqrt)
 
-        states = keep.tile([P, COLS, PACK], BF16, align_bytes=256)
-        by_node = states[:].rearrange("p w t -> p (w t)").bitcast(F32).rearrange(
+        states = early[:, PACK * COLS : 2 * PACK * COLS]
+        by_node = states.bitcast(F32).rearrange(
             "p (u b r) -> p u b r", b=GRAPHS, r=PAIRS
         )
 
@@ -134,7 +137,7 @@ def tile_graphmessagelayer_pa_t_kernel(tc, node_state, positions, We1, be1, We2,
             nc.vector.quantize_mx(
                 out=x_words[:, 0, 0:COLS].bitcast(FP8X4),
                 scales=x_scales[:, 0, 0:COLS],
-                in_=states[:].rearrange("p w t -> p (w t)"),
+                in_=states,
             )
 
         def move_states(to_copy, first_col, from_col, n_cols):
@@ -146,7 +149,7 @@ def tile_graphmessagelayer_pa_t_kernel(tc, node_state, positions, We1, be1, We2,
 
         def copy_states():
             move_states(0, COLS, 0, COPY_COLS - COLS)
-            for copy in range(1, COPIES):
+            for copy in range(COPIES - 1, 0, -1):
                 move_states(copy, 0, copy * GRAPHS, COLS + AHEAD_COLS)
 
         w1_words = keep.tile([P, 2, F], U32, align_bytes=256)
@@ -179,6 +182,10 @@ def tile_graphmessagelayer_pa_t_kernel(tc, node_state, positions, We1, be1, We2,
         apart = keep.tile([P, ROW_BLOCKS, MAX_SHIFT], F32)
         root = keep.tile([P, ROW_BLOCKS, MAX_SHIFT], F32)
 
+        per_feature = keep.tile([P, 2 * F_BLOCKS], F32)
+        w_dist = per_feature[:, 0:F_BLOCKS]
+        bias1 = per_feature[:, F_BLOCKS : 2 * F_BLOCKS]
+
         turn_states(by_vector, 0)
         turn_states(by_scalar, 1)
         turn_states(by_vector, 2)
@@ -195,6 +202,11 @@ def tile_graphmessagelayer_pa_t_kernel(tc, node_state, positions, We1, be1, We2,
             )
         around = keep.tile([P, REACH, COORDS], F32)
         nc.scalar.copy(out=around[:], in_=around_bank[:])
+        g00 = regroup_w1(by_vector, 0, pieces[0])
+        g01 = regroup_w1(by_scalar, 0, pieces[1])
+        quantise_states()
+        copy_states()
+        quantise_w1(g00, 0, pieces[0])
         for q in range(ROW_BLOCKS):
             first = q * BLOCK_NODES
             nc.vector.tensor_tensor(
@@ -203,23 +215,25 @@ def tile_graphmessagelayer_pa_t_kernel(tc, node_state, positions, We1, be1, We2,
                 in1=around[:, first : first + 1, :].to_broadcast([P, MAX_SHIFT, COORDS]),
                 op=ALU.subtract,
             )
-        g00 = regroup_w1(by_vector, 0, pieces[0])
+        g10 = regroup_w1(by_vector, 1, pieces[0])
         nc.vector.tensor_tensor(out=delta_sq[:], in0=delta[:], in1=delta[:], op=ALU.mult)
-        quantise_states()
-        copy_states()
+        quantise_w1(g10, 1, pieces[0])
         nc.vector.tensor_reduce(out=square[:], in_=delta_sq[:], axis=AXIS.X, op=ALU.add)
-        g01 = regroup_w1(by_scalar, 0, pieces[1])
-        quantise_w1(g00, 0, pieces[0])
+        g11 = regroup_w1(by_scalar, 1, pieces[1])
+        quantise_w1(g01, 0, pieces[1])
+        g02 = regroup_w1(by_scalar, 0, pieces[2])
         nc.vector.tensor_scalar_max(out=floored[:], in0=square[:], scalar1=SMALLEST_SQUARE)
         nc.vector.tensor_single_scalar(out=apart[:], in_=square[:], scalar=0.0, op=ALU.is_gt)
         nc.scalar.activation(out=root[:], in_=floored[:], func=ACT.Sqrt)
         nc.scalar.activation(out=warm[:], in_=one[:], func=ACT.Silu)
-        g10 = regroup_w1(by_vector, 1, pieces[0])
-        quantise_w1(g01, 0, pieces[1])
-        quantise_w1(g10, 1, pieces[0])
-        g11 = regroup_w1(by_vector, 1, pieces[1])
-        nc.vector.tensor_tensor(out=dist.rearrange("p s q -> p q s"), in0=root[:], in1=apart[:], op=ALU.mult)
         quantise_w1(g11, 1, pieces[1])
+        nc.vector.tensor_tensor(out=dist.rearrange("p s q -> p q s"), in0=root[:], in1=apart[:], op=ALU.mult)
+        vectors_t = msg_banks.tile([P, P], BF16, tag="msg")
+        nc.tensor.transpose(vectors_t[:], vectors[:], ident_bf16)
+        nc.scalar.copy(out=per_feature[:], in_=vectors_t[:, 0 : 2 * F_BLOCKS])
+        heat = banks.tile([P, COLS], F32, tag="bank")
+        for i in range(5):
+            nc.tensor.matmul(heat[:], lhsT=ident_bf16, rhs=x_rows[:, 0, :], start=True, stop=True)
 
         be2_all = keep.tile([P, ROW_BLOCKS, M], F32)
         w2_grouped = keep.tile([P, F_PASSES, M, PACK], BF16, align_bytes=256)
@@ -251,15 +265,12 @@ def tile_graphmessagelayer_pa_t_kernel(tc, node_state, positions, We1, be1, We2,
             parked = out[GRAPHS - 1 : GRAPHS, 0 : DIST_ROWS // NODES, :, :]
             nc.sync.dma_start(out=parked.rearrange("b i j m -> (b i j) m"), in_=dist_t[0:DIST_ROWS, :])
             flat = parked.rearrange("b i j m -> (b i j m)")
-            for shift in range(MAX_SHIFT - 1, 0, -1):
+            for shift in range(MAX_SHIFT - 2, 0, -1):
                 nc.sync.dma_start(
                     out=dist_rows[:, shift - 1, :],
                     in_=flat[(shift - 1) * COLS : shift * COLS].partition_broadcast(P),
                 )
 
-        per_feature = keep.tile([P, 2 * F_BLOCKS], F32)
-        w_dist = per_feature[:, 0:F_BLOCKS]
-        bias1 = per_feature[:, F_BLOCKS : 2 * F_BLOCKS]
         terms = {}
 
         def start_terms(group):
@@ -279,26 +290,35 @@ def tile_graphmessagelayer_pa_t_kernel(tc, node_state, positions, We1, be1, We2,
                     out=term, in0=dist_row, scalar1=w_col, scalar2=b_col, op0=ALU.mult, op1=ALU.add
                 )
 
-        def node_terms(shift, swapped, c):
+        def node_terms(shift, swapped, c, ts=range(PACK)):
             window = slice((shift // COPIES) * WINDOW_STEP, (shift // COPIES) * WINDOW_STEP + COLS)
             own = (x_words[:, 0, 0:COLS], x_scales[:, 0, 0:COLS])
             partner = (x_words[:, shift % COPIES, window], x_scales[:, shift % COPIES, window])
-            senders = (partner, own) if swapped else (own, partner)
+            parts = [(slice(0, COLS), (partner, own) if swapped else (own, partner))]
+            if shift == MAX_SHIFT:
+                low, high = [
+                    (x_words[:, 0, half], x_scales[:, 0, half]) for half in (slice(0, HALF_COLS), slice(HALF_COLS, COLS))
+                ]
+                parts = [(slice(0, HALF_COLS), (low, high)), (slice(HALF_COLS, COLS), (high, low))]
             accs = []
-            for t in range(PACK):
+            for t in ts:
                 j = c * PACK + t
                 f_cols = slice(j * P, (j + 1) * P)
-                acc = banks.tile([P, COLS], F32, tag="bank")
-                for side in range(2):
-                    nc.tensor.matmul_mx(
-                        out=acc[:],
-                        lhsT=w1_words[:, side, f_cols].bitcast(FP8X4),
-                        lhsT_scale=w1_scales[:, side, f_cols],
-                        rhs=senders[side][0].bitcast(FP8X4),
-                        rhs_scale=senders[side][1],
-                        start=(side == 0),
-                        stop=(side == 1),
-                    )
+                if shift == 0:
+                    acc = msg_banks.tile([P, COLS], F32, tag="msg")
+                else:
+                    acc = banks.tile([P, COLS], F32, tag="bank")
+                for cols, senders in parts:
+                    for side in range(2):
+                        nc.tensor.matmul_mx(
+                            out=acc[:, cols],
+                            lhsT=w1_words[:, side, f_cols].bitcast(FP8X4),
+                            lhsT_scale=w1_scales[:, side, f_cols],
+                            rhs=senders[side][0].bitcast(FP8X4),
+                            rhs_scale=senders[side][1],
+                            start=(side == 0),
+                            stop=(side == 1),
+                        )
                 accs.append(acc)
             return accs
 
@@ -315,15 +335,12 @@ def tile_graphmessagelayer_pa_t_kernel(tc, node_state, positions, We1, be1, We2,
                     op=ALU.add,
                 )
 
-        def add_bias(pre, accs, c):
-            for t in range(PACK):
-                b_col = bias1[:, c * PACK + t : c * PACK + t + 1]
-                if t < PACK // 2:
-                    nc.vector.tensor_scalar_add(out=pre[:, :, t, :], in0=lines(accs[t][:]), scalar1=b_col)
-                else:
-                    nc.scalar.activation(
-                        out=pre[:, :, t, :], in_=lines(accs[t][:]), func=ACT.Identity, bias=b_col, scale=1.0
-                    )
+        def add_bias(j):
+            c, t = divmod(j, PACK)
+            acc = node_terms(0, False, c, (t,))[0]
+            nc.scalar.activation(
+                out=zero_pre[:, :, t, :], in_=lines(acc[:]), func=ACT.Identity, bias=bias1[:, j : j + 1], scale=1.0
+            )
 
         def apply_silu(h, pre, c, cols):
             groups = slice(cols.start // LINE, cols.stop // LINE)
@@ -371,7 +388,7 @@ def tile_graphmessagelayer_pa_t_kernel(tc, node_state, positions, We1, be1, We2,
         def messages(tile, due):
             msg = msg_banks.tile([P, ROW_BLOCKS, M], F32, tag="msg")
             multiply_w2(msg, *codes[tile], 0, ROW_BLOCKS)
-            product = work.tile([P, ROW_BLOCKS, M], F32)
+            product = work.tile([P, ROW_BLOCKS, M], F32, bufs=2)
             nc.scalar.copy(out=product[:], in_=msg[:])
             unfinished.append((due, product, tile))
 
@@ -384,9 +401,9 @@ def tile_graphmessagelayer_pa_t_kernel(tc, node_state, positions, We1, be1, We2,
                 product, tile = entry[1:3]
                 result = work.tile([P, ROW_BLOCKS, M], F32, bufs=4)
                 nc.gpsimd.tensor_tensor(out=result[:], in0=product[:], in1=be2_all[:], op=ALU.add)
-                store(result, *steps[tile * F_PASSES][0:2], nc.sync)
+                store(result, *((0, False) if tile == ZERO else steps[tile * F_PASSES][0:2]), nc.sync)
 
-        groups = [(0,), (MAX_SHIFT,), (MAX_SHIFT - 1,), *((s, s - 1) for s in range(MAX_SHIFT - 2, 0, -2))]
+        groups = [(MAX_SHIFT,), (MAX_SHIFT - 1,), *((s, s - 1) for s in range(MAX_SHIFT - 2, 0, -2))]
         steps = []
         for group, coming in zip(groups, (*groups[1:], ())):
             halves = [
@@ -398,11 +415,19 @@ def tile_graphmessagelayer_pa_t_kernel(tc, node_state, positions, We1, be1, We2,
             share = F_BLOCKS // len(halves)
             for k, half in enumerate(halves):
                 steps.append((*half, coming, range(k * share, (k + 1) * share)))
+        steps[1] = (*steps[1][0:4], range(F_BLOCKS))
 
-        scalar_blocks = {groups[2]: SCALAR_BLOCKS, groups[3]: (3, 6)}
+        scalar_blocks = {groups[1]: SCALAR_BLOCKS, groups[2]: (3, 6)}
+        zero_work = [*range(PACK), F_BLOCKS, *range(PACK, F_BLOCKS), F_BLOCKS + 1]
+        zero_at = {11 + 3 * k: work for k, work in enumerate(zero_work)}
+        zero_quantise = 41
         all_cols = slice(0, COLS)
         halves_of_cols = (slice(0, COLS // 2), slice(COLS // 2, COLS))
         hs = {}
+        zero_pre = early[:].bitcast(F32).rearrange("p (g t i) -> p g t i", t=PACK, i=LINE)
+        zero_h = keep.tile([P, F_PASSES, COLS, PACK], BF16, align_bytes=256)
+        zero_words = keep.tile([P, F_PASSES, COLS], U32, align_bytes=256)
+        zero_scales = keep.tile([P, F_PASSES, COLS], U8, align_bytes=256)
         codes = {}
         last_step = len(steps) - 1
         last_tile = last_step // F_PASSES
@@ -418,29 +443,26 @@ def tile_graphmessagelayer_pa_t_kernel(tc, node_state, positions, We1, be1, We2,
         h_words = work.tile([P, F_PASSES, COLS], U32, align_bytes=256, bufs=4)
         h_scales = work.tile([P, F_PASSES, COLS], U8, align_bytes=256, bufs=4)
         codes[0] = (h_words, h_scales)
-        accs0 = node_terms(0, False, 0)
-        vectors_t = msg_banks.tile([P, P], BF16, tag="msg")
-        nc.tensor.transpose(vectors_t[:], vectors[:], ident_bf16)
-        second_half = []
-        for cols in pieces[2:4]:
-            for side, engine_copy in ((0, by_vector), (1, by_scalar)):
-                second_half.append((regroup_w1(engine_copy, side, cols), side, cols))
-        nc.scalar.copy(out=per_feature[:], in_=vectors_t[:, 0 : 2 * F_BLOCKS])
+        codes[ZERO] = (zero_words, zero_scales)
+        accs0 = node_terms(MAX_SHIFT, False, 0, (0, 1))
         spread_distances(MAX_SHIFT)
-        for piece in second_half:
-            quantise_w1(*piece)
-        prepare_w2()
+        accs0 += node_terms(MAX_SHIFT, False, 0, (2, 3))
         park_distances()
-        pre0 = work.tile([P, COLS // LINE, PACK, LINE], F32, tag="pre")
-        add_bias(pre0, accs0, 0)
-        accs1 = node_terms(0, False, 1)
         start_terms((MAX_SHIFT,))
         for j in range(F_BLOCKS):
-            distance_term((MAX_SHIFT,), j, False)
-        pre1 = work.tile([P, COLS // LINE, PACK, LINE], F32, tag="pre")
-        add_bias(pre1, accs1, 1)
+            distance_term((MAX_SHIFT,), j, j in (0, 1, 4, 5))
+        spread_distances(MAX_SHIFT - 1)
+        g12 = regroup_w1(by_vector, 1, pieces[2])
+        quantise_w1(g02, 0, pieces[2])
+        quantise_w1(g12, 1, pieces[2])
+        g13 = regroup_w1(by_vector, 1, pieces[3])
+        g03 = regroup_w1(by_vector, 0, pieces[3])
+        quantise_w1(g03, 0, pieces[3])
+        quantise_w1(g13, 1, pieces[3])
+        pre0 = work.tile([P, COLS // LINE, PACK, LINE], F32, tag="pre")
+        add_terms(pre0, accs0, terms[MAX_SHIFT], 0, all_cols)
         apply_silu(hs[0], pre0, 0, all_cols)
-        apply_silu(hs[0], pre1, 1, all_cols)
+        prepare_w2()
         be2_bank = msg_banks.tile([P, M], F32, tag="msg")
         nc.tensor.matmul(
             be2_bank[:],
@@ -451,7 +473,8 @@ def tile_graphmessagelayer_pa_t_kernel(tc, node_state, positions, We1, be1, We2,
         )
         nc.scalar.copy(out=be2_all[:], in_=be2_bank[:].unsqueeze(1).to_broadcast([P, ROW_BLOCKS, M]))
 
-        for g in range(F_PASSES, len(steps)):
+        early = False
+        for g in range(1, len(steps)):
             shift, swapped, c, coming, blocks = steps[g]
             tile = g // F_PASSES
             if c == 0:
@@ -470,6 +493,9 @@ def tile_graphmessagelayer_pa_t_kernel(tc, node_state, positions, We1, be1, We2,
             accs = node_terms(shift, swapped, c)
             if g < last_step:
                 add_terms(pre, accs, terms[shift], c, all_cols)
+                early = g > last_step - 3 and g in multiply_at
+                if early:
+                    messages(multiply_at[g], min(g + ADD_LAG, last_step))
                 apply_silu(hs[tile], pre, c, all_cols)
             else:
                 msg = msg_banks.tile([P, ROW_BLOCKS, M], F32, tag="msg")
@@ -482,11 +508,20 @@ def tile_graphmessagelayer_pa_t_kernel(tc, node_state, positions, We1, be1, We2,
                 nc.vector.tensor_tensor(out=result[:], in0=msg[:], in1=be2_all[:], op=ALU.add)
                 finish_messages(g)
                 store(result, *steps[g - F_PASSES][0:2], nc.sync)
+            if g in zero_at:
+                if zero_at[g] < F_BLOCKS:
+                    add_bias(zero_at[g])
+                else:
+                    apply_silu(zero_h, zero_pre, zero_at[g] - F_BLOCKS, all_cols)
             if g in quantise_at:
                 tile = quantise_at[g]
                 quantise_h(hs[tile], *codes[tile], 0, F_PASSES, all_cols)
-            if g in multiply_at:
+            if g in multiply_at and not early:
                 messages(multiply_at[g], min(g + ADD_LAG, last_step))
+            if g == zero_quantise:
+                quantise_h(zero_h, *codes[ZERO], 0, F_PASSES, all_cols)
+            if g == zero_quantise + 2:
+                messages(ZERO, g + ADD_LAG)
 
         quantise_h(hs[last_tile], *codes[last_tile], 0, 1, all_cols)
         result = work.tile([P, ROW_BLOCKS, M], F32, bufs=4)

@@ -42,6 +42,8 @@ REACH = (ROW_BLOCKS - 1) * BLOCK_NODES + MAX_SHIFT + 1
 SMALLEST_SQUARE = 2.0**-100
 
 SCALAR_BLOCKS = (3, 4)
+GPSIMD_TERMS = {0: (0, 1), 2: (2, 4), 4: (5, 6), 6: (7,)}
+SCALAR_TERMS = {1: 3}
 ZERO = -1
 DIST_ROWS = MAX_SHIFT * ROW_BLOCKS
 LINE = 4
@@ -450,7 +452,7 @@ def tile_graphmessagelayer_pa_t_kernel(tc, node_state, positions, We1, be1, We2,
         park_distances()
         start_terms((MAX_SHIFT,))
         for j in range(F_BLOCKS):
-            distance_term((MAX_SHIFT,), j, j in (0, 1, 4, 5))
+            distance_term((MAX_SHIFT,), j, j in (0, 1, 2, 4, 5, 6))
         spread_distances(MAX_SHIFT - 1)
         g12 = regroup_w1(by_vector, 1, pieces[2])
         quantise_w1(g02, 0, pieces[2])
@@ -474,6 +476,8 @@ def tile_graphmessagelayer_pa_t_kernel(tc, node_state, positions, We1, be1, We2,
         nc.scalar.copy(out=be2_all[:], in_=be2_bank[:].unsqueeze(1).to_broadcast([P, ROW_BLOCKS, M]))
 
         early = False
+        first_pair_step = 6
+        held = [g for g in quantise_at if first_pair_step <= g < last_step - 5]
         for g in range(1, len(steps)):
             shift, swapped, c, coming, blocks = steps[g]
             tile = g // F_PASSES
@@ -483,12 +487,15 @@ def tile_graphmessagelayer_pa_t_kernel(tc, node_state, positions, We1, be1, We2,
                 h_words = work.tile([P, F_PASSES, COLS], U32, align_bytes=256, bufs=4)
                 h_scales = work.tile([P, F_PASSES, COLS], U8, align_bytes=256, bufs=4)
                 codes[tile] = (h_words, h_scales)
-            finish_messages(g)
-            if coming:
+            if g not in held:
+                finish_messages(g)
+            if coming and g < first_pair_step:
                 if 0 in blocks:
                     start_terms(coming)
                 for j in blocks:
                     distance_term(coming, j, j in scalar_blocks.get(coming, ()))
+            elif coming and (g - first_pair_step) % 8 in SCALAR_TERMS:
+                distance_term(coming, SCALAR_TERMS[(g - first_pair_step) % 8], True)
             pre = work.tile([P, COLS // LINE, PACK, LINE], F32, tag="pre")
             accs = node_terms(shift, swapped, c)
             if g < last_step:
@@ -516,6 +523,15 @@ def tile_graphmessagelayer_pa_t_kernel(tc, node_state, positions, We1, be1, We2,
             if g in quantise_at:
                 tile = quantise_at[g]
                 quantise_h(hs[tile], *codes[tile], 0, F_PASSES, all_cols)
+                if g in held:
+                    nc.gpsimd.memset(hs[tile][:, 0, 0, :], 0.0)
+                    if coming:
+                        k = (g - first_pair_step) % 8
+                        if k == 0:
+                            start_terms(coming)
+                        for j in GPSIMD_TERMS[k]:
+                            distance_term(coming, j, False)
+                    finish_messages(g)
             if g in multiply_at and not early:
                 messages(multiply_at[g], min(g + ADD_LAG, last_step))
             if g == zero_quantise:

@@ -421,8 +421,8 @@ def tile_graphmessagelayer_pa_t_kernel(tc, node_state, positions, We1, be1, We2,
 
         scalar_blocks = {groups[1]: SCALAR_BLOCKS, groups[2]: (3, 6)}
         zero_work = [*range(PACK), F_BLOCKS, *range(PACK, F_BLOCKS), F_BLOCKS + 1]
-        zero_at = {11 + 3 * k: work for k, work in enumerate(zero_work)}
-        zero_quantise = 41
+        zero_at = {11 + 4 * k: work for k, work in enumerate(zero_work)}
+        zero_quantise = 51
         all_cols = slice(0, COLS)
         halves_of_cols = (slice(0, COLS // 2), slice(COLS // 2, COLS))
         hs = {}
@@ -452,7 +452,7 @@ def tile_graphmessagelayer_pa_t_kernel(tc, node_state, positions, We1, be1, We2,
         park_distances()
         start_terms((MAX_SHIFT,))
         for j in range(F_BLOCKS):
-            distance_term((MAX_SHIFT,), j, j in (0, 1, 2, 4, 5, 6))
+            distance_term((MAX_SHIFT,), j, j in (0, 1, 4, 5))
         spread_distances(MAX_SHIFT - 1)
         g12 = regroup_w1(by_vector, 1, pieces[2])
         quantise_w1(g02, 0, pieces[2])
@@ -514,7 +514,7 @@ def tile_graphmessagelayer_pa_t_kernel(tc, node_state, positions, We1, be1, We2,
                 result = work.tile([P, ROW_BLOCKS, M], F32, bufs=4)
                 nc.vector.tensor_tensor(out=result[:], in0=msg[:], in1=be2_all[:], op=ALU.add)
                 finish_messages(g)
-                store(result, *steps[g - F_PASSES][0:2], nc.sync)
+                store(result, *steps[g - F_PASSES][0:2], nc.gpsimd)
             if g in zero_at:
                 if zero_at[g] < F_BLOCKS:
                     add_bias(zero_at[g])
@@ -541,11 +541,14 @@ def tile_graphmessagelayer_pa_t_kernel(tc, node_state, positions, We1, be1, We2,
 
         quantise_h(hs[last_tile], *codes[last_tile], 0, 1, all_cols)
         result = work.tile([P, ROW_BLOCKS, M], F32, bufs=4)
+        last_msgs = []
         for half, cols in enumerate(halves_of_cols):
             q0 = half * ROW_BLOCKS // 2
             q1 = q0 + ROW_BLOCKS // 2
             quantise_h(hs[last_tile], *codes[last_tile], 1, 2, cols)
             msg = banks.tile([P, ROW_BLOCKS // 2, M], F32, tag="bank")
             multiply_w2(msg, *codes[last_tile], q0, q1)
+            last_msgs.append((msg, q0, q1))
+        for msg, q0, q1 in last_msgs:
             nc.vector.tensor_tensor(out=result[:, q0:q1, :], in0=msg[:], in1=be2_all[:, q0:q1, :], op=ALU.add)
         store(result, *steps[last_step][0:2], nc.gpsimd)

@@ -421,8 +421,8 @@ def tile_graphmessagelayer_pa_t_kernel(tc, node_state, positions, We1, be1, We2,
 
         scalar_blocks = {groups[1]: SCALAR_BLOCKS, groups[2]: (3, 6)}
         zero_work = [*range(PACK), F_BLOCKS, *range(PACK, F_BLOCKS), F_BLOCKS + 1]
-        zero_at = {11 + 4 * k: work for k, work in enumerate(zero_work)}
-        zero_quantise = 51
+        zero_at = {11 + 3 * k: work for k, work in enumerate(zero_work)}
+        zero_quantise = 41
         all_cols = slice(0, COLS)
         halves_of_cols = (slice(0, COLS // 2), slice(COLS // 2, COLS))
         hs = {}
@@ -494,7 +494,7 @@ def tile_graphmessagelayer_pa_t_kernel(tc, node_state, positions, We1, be1, We2,
                     start_terms(coming)
                 for j in blocks:
                     distance_term(coming, j, j in scalar_blocks.get(coming, ()))
-            elif coming and (g - first_pair_step) % 8 in SCALAR_TERMS:
+            elif coming and g >= 38 and (g - first_pair_step) % 8 in SCALAR_TERMS:
                 distance_term(coming, SCALAR_TERMS[(g - first_pair_step) % 8], True)
             pre = work.tile([P, COLS // LINE, PACK, LINE], F32, tag="pre")
             accs = node_terms(shift, swapped, c)
@@ -529,7 +529,7 @@ def tile_graphmessagelayer_pa_t_kernel(tc, node_state, positions, We1, be1, We2,
                         k = (g - first_pair_step) % 8
                         if k == 0:
                             start_terms(coming)
-                        for j in GPSIMD_TERMS[k]:
+                        for j in GPSIMD_TERMS[k] if g >= 38 else (k, k + 1):
                             distance_term(coming, j, False)
                     finish_messages(g)
             if g in multiply_at and not early:

from contextlib import ExitStack

import concourse.mybir as mybir
from concourse.masks import make_identity

F32 = mybir.dt.float32
BF16 = mybir.dt.bfloat16
U32 = mybir.dt.uint32
U8 = mybir.dt.uint8
I32 = mybir.dt.int32
FP8X4 = mybir.dt.float8_e4m3fn_x4
ALU = mybir.AluOpType
ACT = mybir.ActivationFunctionType
AXIS = mybir.AxisListType

P = 128
PACK = 4
PAIRS = PACK // 2
K_PASS = P * PACK

GRAPHS = 16
NODES = 32
COORDS = 3
H = 512
F = 1024
M = 128

COLS = NODES * GRAPHS
F_BLOCKS = F // P
F_PASSES = F // K_PASS
ROW_BLOCKS = COLS // P
BLOCK_NODES = P // GRAPHS
MAX_SHIFT = NODES // 2

HALF_COLS = COLS // 2
COPIES = 4
WINDOW_STEP = COPIES * GRAPHS
AHEAD_COLS = MAX_SHIFT // COPIES * WINDOW_STEP
COPY_COLS = COLS + AHEAD_COLS + WINDOW_STEP

REACH = (ROW_BLOCKS - 1) * BLOCK_NODES + MAX_SHIFT + 1
SMALLEST_SQUARE = 2.0**-100

SCALAR_BLOCKS = (3, 4)
GPSIMD_TERMS = {0: (0, 1), 2: (2, 4), 4: (5, 6), 6: (7,)}
SCALAR_TERMS = {1: 3}
ZERO = -1
DIST_ROWS = MAX_SHIFT * ROW_BLOCKS
LINE = 4
PIECE = K_PASS // 2
BE2_ROW = 32
QUANTISE_LAG = 3
ADD_LAG = 1
MESSAGE_LAG = 4

FLOPS = 2 * GRAPHS * NODES * H * 2 * F + 2 * GRAPHS * NODES * NODES * F * M


def regroup(engine_copy, grouped, planes):
    engine_copy(
        out=grouped.rearrange("p (g i) t -> p g t i", i=4),
        in_=planes.rearrange("p t (g i) -> p g t i", i=4),
    )


def tile_graphmessagelayer_pa_t_kernel(tc, node_state, positions, We1, be1, We2, be2, out):
    nc = tc.nc
    with ExitStack() as ctx:
        keep = ctx.enter_context(tc.tile_pool(name="keep", bufs=1))
        stage = ctx.enter_context(tc.tile_pool(name="stage", bufs=2))
        work = ctx.enter_context(tc.tile_pool(name="work", bufs=3))
        banks = ctx.enter_context(tc.psum_pool(name="banks", bufs=6))
        msg_banks = ctx.enter_context(tc.psum_pool(name="msg_banks", bufs=2))
        ctx.enter_context(tc.manual_schedule())

        pos_rows = keep.tile([P, 2, NODES * COORDS], BF16)
        nc.vector.memset(pos_rows[:], 0.0)
        vectors = keep.tile([P, P], BF16)
        nc.vector.memset(vectors[:], 0.0)
        nc.scalar.dma_start(
            out=vectors[0:F_BLOCKS, :], in_=We1[2 * H : 2 * H + 1, :].rearrange("o (j p) -> (o j) p", p=P)
        )
        nc.scalar.dma_start(out=vectors[F_BLOCKS : 2 * F_BLOCKS, :], in_=be1.rearrange("(j p) -> j p", p=P))
        nc.scalar.dma_start(out=vectors[BE2_ROW : BE2_ROW + 1, :], in_=be2.unsqueeze(0))

        early = keep.tile([P, 2 * PACK * COLS], BF16, align_bytes=256)
        x_rows = early[:, 0 : PACK * COLS].rearrange("p (g k) -> p g k", k=H)
        x_view = node_state.rearrange("(g bl) u k -> (bl u) g k", bl=4)
        for g in (0, 2):
            nc.sync.dma_start(out=x_rows[:, g : g + 2, :], in_=x_view[:, g : g + 2, :])
        for copy in range(2):
            nc.sync.dma_start(out=pos_rows[0:GRAPHS, copy, :], in_=positions.rearrange("b u c -> b (u c)"))
        w1_space = stage.tile([P, 4 * PACK * F], BF16, align_bytes=64, tag="term")
        w1_rows = w1_space[:, 0 : 2 * PACK * F].rearrange("p (j f) -> p j f", f=F)
        w1_view = [We1[side * H : (side + 1) * H, :].rearrange("(p t) f -> p t f", t=PACK) for side in range(2)]
        for c in range(F_PASSES):
            f_half = slice(c * K_PASS, (c + 1) * K_PASS)
            for side in range(2):
                blocks = slice(side * PACK, (side + 1) * PACK)
                nc.sync.dma_start(out=w1_rows[:, blocks, f_half], in_=w1_view[side][:, :, f_half])
        w2_rows = keep.tile([P, F_BLOCKS, M], BF16)
        nc.sync.dma_start(out=w2_rows[:], in_=We2.rearrange("(j p) m -> p j m", p=P))

        dist_square = keep.tile([P, P], F32)
        nc.vector.memset(dist_square[:], 0.0)

        left = P - GRAPHS
        wide = keep.tile([P, left + P], BF16)
        nc.vector.memset(wide[:, 0:left], 0.0)
        make_identity(nc, wide[:, left : left + P])
        ident_bf16 = wide[:, left : left + P]
        ident_f32 = keep.tile([P, P], F32)
        make_identity(nc, ident_f32[:])
        x_words = keep.tile([P, COPIES, COPY_COLS], U32, align_bytes=256)
        x_scales = keep.tile([P, COPIES, COPY_COLS], U8, align_bytes=256)
        nc.gpsimd.memset(x_scales[:].rearrange("p c w -> p (c w)").bitcast(I32), 0)
        one = keep.tile([P, 1], F32)
        nc.vector.memset(one[:], 1.0)
        warm = keep.tile([P, 1], F32)
        nc.scalar.activation(out=warm[:], in_=one[:], func=ACT.Sqrt)

        states = early[:, PACK * COLS : 2 * PACK * COLS]
        by_node = states.bitcast(F32).rearrange(
            "p (u b r) -> p u b r", b=GRAPHS, r=PAIRS
        )

        def turn_states(engine_copy, g):
            x_t = banks.tile([P, PAIRS, P], F32, tag="bank")
            x_pairs = x_rows[:, g, :].bitcast(F32)
            for r in range(PAIRS):
                nc.tensor.transpose(x_t[:, r, :], x_pairs[:, r : H // 2 : PAIRS], ident_f32[:])
            engine_copy(
                out=by_node[:, :, 4 * g : 4 * g + 4, :], in_=x_t[:].rearrange("p r (bl u) -> p u bl r", u=NODES)
            )

        by_vector = nc.vector.tensor_copy
        by_scalar = nc.scalar.copy
        def quantise_states():
            nc.vector.quantize_mx(
                out=x_words[:, 0, 0:COLS].bitcast(FP8X4),
                scales=x_scales[:, 0, 0:COLS],
                in_=states,
            )

        def move_states(to_copy, first_col, from_col, n_cols):
            for rows in (x_words, x_scales):
                nc.sync.dma_start(
                    out=rows[:, to_copy, first_col : first_col + n_cols].bitcast(I32),
                    in_=rows[:, 0, from_col : from_col + n_cols].bitcast(I32),
                )

        def copy_states():
            move_states(0, COLS, 0, COPY_COLS - COLS)
            for copy in range(COPIES - 1, 0, -1):
                move_states(copy, 0, copy * GRAPHS, COLS + AHEAD_COLS)

        w1_words = keep.tile([P, 2, F], U32, align_bytes=256)
        w1_scales = keep.tile([P, 2, F], U8, align_bytes=256)

        def regroup_w1(engine_copy, side, cols):
            first = 2 * PACK * F + (side * F + cols.start) * PACK
            grouped = w1_space[:, first : first + PIECE * PACK]
            regroup(
                engine_copy,
                grouped.rearrange("p (w t) -> p w t", t=PACK),
                w1_rows[:, side * PACK : (side + 1) * PACK, cols],
            )
            return grouped

        def quantise_w1(grouped, side, cols):
            nc.vector.quantize_mx(
                out=w1_words[:, side, cols].bitcast(FP8X4),
                scales=w1_scales[:, side, cols],
                in_=grouped,
            )

        pieces = [slice(k * PIECE, (k + 1) * PIECE) for k in range(F // PIECE)]

        dist = dist_square[:, 0:DIST_ROWS].rearrange("p (s q) -> p s q", q=ROW_BLOCKS)
        delta = keep.tile([P, ROW_BLOCKS, MAX_SHIFT, COORDS], F32)
        delta_sq = keep.tile([P, ROW_BLOCKS, MAX_SHIFT, COORDS], F32)
        square = keep.tile([P, ROW_BLOCKS, MAX_SHIFT], F32)
        floored = keep.tile([P, ROW_BLOCKS, MAX_SHIFT], F32)
        apart = keep.tile([P, ROW_BLOCKS, MAX_SHIFT], F32)
        root = keep.tile([P, ROW_BLOCKS, MAX_SHIFT], F32)

        per_feature = keep.tile([P, 2 * F_BLOCKS], F32)
        w_dist = per_feature[:, 0:F_BLOCKS]
        bias1 = per_feature[:, F_BLOCKS : 2 * F_BLOCKS]

        turn_states(by_vector, 0)
        turn_states(by_scalar, 1)
        turn_states(by_vector, 2)
        turn_states(by_scalar, 3)
        around_bank = msg_banks.tile([P, REACH, COORDS], F32, tag="msg")
        pos_round = pos_rows[:].rearrange("p r x -> p (r x)")
        for lane in range(BLOCK_NODES):
            nc.tensor.matmul(
                around_bank[:].rearrange("p n x -> p (n x)"),
                lhsT=wide[:, left - lane * GRAPHS : left - lane * GRAPHS + P],
                rhs=pos_round[:, lane * COORDS : (lane + REACH) * COORDS],
                start=(lane == 0),
                stop=(lane == BLOCK_NODES - 1),
            )
        around = keep.tile([P, REACH, COORDS], F32)
        nc.scalar.copy(out=around[:], in_=around_bank[:])
        g00 = regroup_w1(by_vector, 0, pieces[0])
        g01 = regroup_w1(by_scalar, 0, pieces[1])
        quantise_states()
        copy_states()
        quantise_w1(g00, 0, pieces[0])
        for q in range(ROW_BLOCKS):
            first = q * BLOCK_NODES
            nc.vector.tensor_tensor(
                out=delta[:, q],
                in0=around[:, first + 1 : first + 1 + MAX_SHIFT, :],
                in1=around[:, first : first + 1, :].to_broadcast([P, MAX_SHIFT, COORDS]),
                op=ALU.subtract,
            )
        g10 = regroup_w1(by_vector, 1, pieces[0])
        nc.vector.tensor_tensor(out=delta_sq[:], in0=delta[:], in1=delta[:], op=ALU.mult)
        quantise_w1(g10, 1, pieces[0])
        nc.vector.tensor_reduce(out=square[:], in_=delta_sq[:], axis=AXIS.X, op=ALU.add)
        g11 = regroup_w1(by_scalar, 1, pieces[1])
        quantise_w1(g01, 0, pieces[1])
        g02 = regroup_w1(by_scalar, 0, pieces[2])
        nc.vector.tensor_scalar_max(out=floored[:], in0=square[:], scalar1=SMALLEST_SQUARE)
        nc.vector.tensor_single_scalar(out=apart[:], in_=square[:], scalar=0.0, op=ALU.is_gt)
        nc.scalar.activation(out=root[:], in_=floored[:], func=ACT.Sqrt)
        nc.scalar.activation(out=warm[:], in_=one[:], func=ACT.Silu)
        quantise_w1(g11, 1, pieces[1])
        nc.vector.tensor_tensor(out=dist.rearrange("p s q -> p q s"), in0=root[:], in1=apart[:], op=ALU.mult)
        vectors_t = msg_banks.tile([P, P], BF16, tag="msg")
        nc.tensor.transpose(vectors_t[:], vectors[:], ident_bf16)
        nc.scalar.copy(out=per_feature[:], in_=vectors_t[:, 0 : 2 * F_BLOCKS])
        heat = banks.tile([P, COLS], F32, tag="bank")
        for i in range(5):
            nc.tensor.matmul(heat[:], lhsT=ident_bf16, rhs=x_rows[:, 0, :], start=True, stop=True)

        be2_all = keep.tile([P, ROW_BLOCKS, M], F32)
        w2_grouped = keep.tile([P, F_PASSES, M, PACK], BF16, align_bytes=256)
        w2_words = keep.tile([P, F_PASSES * M], U32, align_bytes=256)
        w2_scales = keep.tile([P, F_PASSES * M], U8, align_bytes=256)

        def prepare_w2():
            for c in range(F_PASSES):
                regroup(nc.vector.tensor_copy, w2_grouped[:, c], w2_rows[:, c * PACK : (c + 1) * PACK, :])
            nc.vector.quantize_mx(
                out=w2_words[:].bitcast(FP8X4),
                scales=w2_scales[:],
                in_=w2_grouped[:].rearrange("p c m t -> p (c m t)"),
            )

        dist_rows = keep.tile([P, MAX_SHIFT, COLS], F32)

        def spread_distances(shift):
            spread = msg_banks.tile([P, ROW_BLOCKS, P], F32, tag="msg")
            for q in range(ROW_BLOCKS):
                nc.tensor.transpose(spread[:, q, :], dist[:, shift - 1, q : q + 1].to_broadcast([P, P]), ident_f32[:])
            nc.scalar.copy(out=dist_rows[:, shift - 1, :], in_=spread[:].rearrange("p q k -> p (q k)"))

        def park_distances():
            turned = msg_banks.tile([P, P], F32, tag="msg")
            nc.tensor.transpose(turned[:], dist_square[:], ident_f32[:])
            dist_t = keep.tile([P, P], F32)
            nc.scalar.copy(out=dist_t[:], in_=turned[:])
            parked = out[GRAPHS - 1 : GRAPHS, 0 : DIST_ROWS // NODES, :, :]
            nc.sync.dma_start(out=parked.rearrange("b i j m -> (b i j) m"), in_=dist_t[0:DIST_ROWS, :])
            flat = parked.rearrange("b i j m -> (b i j m)")
            for shift in range(MAX_SHIFT - 2, 0, -1):
                nc.sync.dma_start(
                    out=dist_rows[:, shift - 1, :],
                    in_=flat[(shift - 1) * COLS : shift * COLS].partition_broadcast(P),
                )

        terms = {}

        def start_terms(group):
            room = stage.tile([P, F_BLOCKS, len(group), COLS], F32, align_bytes=64, tag="term")
            for k, shift in enumerate(reversed(group)):
                terms[shift] = room[:, :, k, :]
            terms[group] = room

        def distance_term(group, j, on_scalar):
            term = terms[group][:, j].rearrange("p s e -> p (s e)")
            dist_row = dist_rows[:, group[-1] - 1 : group[0], :].rearrange("p s e -> p (s e)")
            w_col, b_col = w_dist[:, j : j + 1], bias1[:, j : j + 1]
            if on_scalar:
                nc.scalar.activation(out=term, in_=dist_row, func=ACT.Identity, scale=w_col, bias=b_col)
            else:
                nc.gpsimd.tensor_scalar(
                    out=term, in0=dist_row, scalar1=w_col, scalar2=b_col, op0=ALU.mult, op1=ALU.add
                )

        def node_terms(shift, swapped, c, ts=range(PACK)):
            window = slice((shift // COPIES) * WINDOW_STEP, (shift // COPIES) * WINDOW_STEP + COLS)
            own = (x_words[:, 0, 0:COLS], x_scales[:, 0, 0:COLS])
            partner = (x_words[:, shift % COPIES, window], x_scales[:, shift % COPIES, window])
            parts = [(slice(0, COLS), (partner, own) if swapped else (own, partner))]
            if shift == MAX_SHIFT:
                low, high = [
                    (x_words[:, 0, half], x_scales[:, 0, half]) for half in (slice(0, HALF_COLS), slice(HALF_COLS, COLS))
                ]
                parts = [(slice(0, HALF_COLS), (low, high)), (slice(HALF_COLS, COLS), (high, low))]
            accs = []
            for t in ts:
                j = c * PACK + t
                f_cols = slice(j * P, (j + 1) * P)
                if shift == 0:
                    acc = msg_banks.tile([P, COLS], F32, tag="msg")
                else:
                    acc = banks.tile([P, COLS], F32, tag="bank")
                for cols, senders in parts:
                    for side in range(2):
                        nc.tensor.matmul_mx(
                            out=acc[:, cols],
                            lhsT=w1_words[:, side, f_cols].bitcast(FP8X4),
                            lhsT_scale=w1_scales[:, side, f_cols],
                            rhs=senders[side][0].bitcast(FP8X4),
                            rhs_scale=senders[side][1],
                            start=(side == 0),
                            stop=(side == 1),
                        )
                accs.append(acc)
            return accs

        def lines(plane):
            return plane.rearrange("p (g i) -> p g i", i=LINE)

        def add_terms(pre, accs, term, c, cols):
            groups = slice(cols.start // LINE, cols.stop // LINE)
            for t in range(PACK):
                nc.vector.tensor_tensor(
                    out=pre[:, groups, t, :],
                    in0=lines(accs[t][:, cols]),
                    in1=lines(term[:, c * PACK + t, cols]),
                    op=ALU.add,
                )

        def add_bias(j):
            c, t = divmod(j, PACK)
            acc = node_terms(0, False, c, (t,))[0]
            nc.scalar.activation(
                out=zero_pre[:, :, t, :], in_=lines(acc[:]), func=ACT.Identity, bias=bias1[:, j : j + 1], scale=1.0
            )

        def apply_silu(h, pre, c, cols):
            groups = slice(cols.start // LINE, cols.stop // LINE)
            nc.scalar.activation(
                out=h[:, c, cols, :].rearrange("p (g i) t -> p g t i", i=LINE), in_=pre[:, groups], func=ACT.Silu
            )

        def quantise_h(h, h_words, h_scales, c0, c1, cols):
            nc.vector.quantize_mx(
                out=h_words[:, c0:c1, cols].rearrange("p c w -> p (c w)").bitcast(FP8X4),
                scales=h_scales[:, c0:c1, cols].rearrange("p c w -> p (c w)"),
                in_=h[:, c0:c1, cols, :].rearrange("p c w t -> p (c w t)"),
            )

        def multiply_w2(msg, h_words, h_scales, q0, q1):
            for q in range(q0, q1):
                edges = slice(q * P, (q + 1) * P)
                for c in range(F_PASSES):
                    nc.tensor.matmul_mx(
                        out=msg[:, q - q0, :],
                        lhsT=h_words[:, c, edges].bitcast(FP8X4),
                        lhsT_scale=h_scales[:, c, edges],
                        rhs=w2_words[:, c * M : (c + 1) * M].bitcast(FP8X4),
                        rhs_scale=w2_scales[:, c * M : (c + 1) * M],
                        start=(c == 0),
                        stop=(c == F_PASSES - 1),
                    )

        out_rows = out.rearrange("b i j m -> b (i j) m")

        def store(result, shift, swapped, round_queue):
            row_step = BLOCK_NODES * (NODES + 1)
            for lane in range(BLOCK_NODES):
                rows = slice(lane * GRAPHS, (lane + 1) * GRAPHS)
                straight = (NODES - 1 - lane - shift) // BLOCK_NODES + 1
                for queue, b0, b1, v_minus_u in (
                    (nc.sync, 0, straight, shift),
                    (round_queue, straight, ROW_BLOCKS, shift - NODES),
                ):
                    if b1 > b0:
                        first = (b0 * BLOCK_NODES + lane) * (NODES + 1) + v_minus_u * (NODES if swapped else 1)
                        last = first + (b1 - b0 - 1) * row_step
                        queue.dma_start(out=out_rows[:, first : last + 1 : row_step, :], in_=result[rows, b0:b1, :])

        def messages(tile, due):
            msg = msg_banks.tile([P, ROW_BLOCKS, M], F32, tag="msg")
            multiply_w2(msg, *codes[tile], 0, ROW_BLOCKS)
            product = work.tile([P, ROW_BLOCKS, M], F32, bufs=2)
            nc.scalar.copy(out=product[:], in_=msg[:])
            unfinished.append((due, product, tile))

        unfinished = []

        def finish_messages(step):
            while unfinished and unfinished[0][0] <= step:
                entry = unfinished[0]
                unfinished.remove(entry)
                product, tile = entry[1:3]
                result = work.tile([P, ROW_BLOCKS, M], F32, bufs=4)
                nc.gpsimd.tensor_tensor(out=result[:], in0=product[:], in1=be2_all[:], op=ALU.add)
                store(result, *((0, False) if tile == ZERO else steps[tile * F_PASSES][0:2]), nc.sync)

        groups = [(MAX_SHIFT,), (MAX_SHIFT - 1,), *((s, s - 1) for s in range(MAX_SHIFT - 2, 0, -2))]
        steps = []
        for group, coming in zip(groups, (*groups[1:], ())):
            halves = [
                (shift, swapped, c)
                for shift in group
                for swapped in ((False, True) if 0 < shift < MAX_SHIFT else (False,))
                for c in range(F_PASSES)
            ]
            share = F_BLOCKS // len(halves)
            for k, half in enumerate(halves):
                steps.append((*half, coming, range(k * share, (k + 1) * share)))
        steps[1] = (*steps[1][0:4], range(F_BLOCKS))

        scalar_blocks = {groups[1]: SCALAR_BLOCKS, groups[2]: (3, 6)}
        zero_work = [*range(PACK), F_BLOCKS, *range(PACK, F_BLOCKS), F_BLOCKS + 1]
        zero_at = {11 + 3 * k: work for k, work in enumerate(zero_work)}
        zero_quantise = 41
        all_cols = slice(0, COLS)
        halves_of_cols = (slice(0, COLS // 2), slice(COLS // 2, COLS))
        hs = {}
        zero_pre = early[:].bitcast(F32).rearrange("p (g t i) -> p g t i", t=PACK, i=LINE)
        zero_h = keep.tile([P, F_PASSES, COLS, PACK], BF16, align_bytes=256)
        zero_words = keep.tile([P, F_PASSES, COLS], U32, align_bytes=256)
        zero_scales = keep.tile([P, F_PASSES, COLS], U8, align_bytes=256)
        codes = {}
        last_step = len(steps) - 1
        last_tile = last_step // F_PASSES

        quantise_at, multiply_at = {}, {}
        for tile in range(last_tile):
            second_half_step = tile * F_PASSES + 1
            quantise_at[min(second_half_step + QUANTISE_LAG, last_step - last_tile + tile)] = tile
            if tile < last_tile - 1:
                multiply_at[min(second_half_step + MESSAGE_LAG, last_step - last_tile + tile + 1)] = tile
        h = work.tile([P, F_PASSES, COLS, PACK], BF16, align_bytes=256)
        hs[0] = h
        h_words = work.tile([P, F_PASSES, COLS], U32, align_bytes=256, bufs=4)
        h_scales = work.tile([P, F_PASSES, COLS], U8, align_bytes=256, bufs=4)
        codes[0] = (h_words, h_scales)
        codes[ZERO] = (zero_words, zero_scales)
        accs0 = node_terms(MAX_SHIFT, False, 0, (0, 1))
        spread_distances(MAX_SHIFT)
        accs0 += node_terms(MAX_SHIFT, False, 0, (2, 3))
        park_distances()
        start_terms((MAX_SHIFT,))
        for j in range(F_BLOCKS):
            distance_term((MAX_SHIFT,), j, j in (0, 1, 4, 5))
        spread_distances(MAX_SHIFT - 1)
        g12 = regroup_w1(by_vector, 1, pieces[2])
        quantise_w1(g02, 0, pieces[2])
        quantise_w1(g12, 1, pieces[2])
        g13 = regroup_w1(by_vector, 1, pieces[3])
        g03 = regroup_w1(by_vector, 0, pieces[3])
        quantise_w1(g03, 0, pieces[3])
        quantise_w1(g13, 1, pieces[3])
        pre0 = work.tile([P, COLS // LINE, PACK, LINE], F32, tag="pre")
        add_terms(pre0, accs0, terms[MAX_SHIFT], 0, all_cols)
        apply_silu(hs[0], pre0, 0, all_cols)
        prepare_w2()
        be2_bank = msg_banks.tile([P, M], F32, tag="msg")
        nc.tensor.matmul(
            be2_bank[:],
            lhsT=ident_bf16[:, BE2_ROW : BE2_ROW + 1].to_broadcast([P, P]),
            rhs=vectors[:],
            start=True,
            stop=True,
        )
        nc.scalar.copy(out=be2_all[:], in_=be2_bank[:].unsqueeze(1).to_broadcast([P, ROW_BLOCKS, M]))

        early = False
        first_pair_step = 6
        held = [g for g in quantise_at if first_pair_step <= g < last_step - 5]
        for g in range(1, len(steps)):
            shift, swapped, c, coming, blocks = steps[g]
            tile = g // F_PASSES
            if c == 0:
                h = work.tile([P, F_PASSES, COLS, PACK], BF16, align_bytes=256)
                hs[tile] = h
                h_words = work.tile([P, F_PASSES, COLS], U32, align_bytes=256, bufs=4)
                h_scales = work.tile([P, F_PASSES, COLS], U8, align_bytes=256, bufs=4)
                codes[tile] = (h_words, h_scales)
            if g not in held:
                finish_messages(g)
            if coming and g < first_pair_step:
                if 0 in blocks:
                    start_terms(coming)
                for j in blocks:
                    distance_term(coming, j, j in scalar_blocks.get(coming, ()))
            elif coming and g >= 38 and (g - first_pair_step) % 8 in SCALAR_TERMS:
                distance_term(coming, SCALAR_TERMS[(g - first_pair_step) % 8], True)
            pre = work.tile([P, COLS // LINE, PACK, LINE], F32, tag="pre")
            accs = node_terms(shift, swapped, c)
            if g < last_step:
                add_terms(pre, accs, terms[shift], c, all_cols)
                early = g > last_step - 3 and g in multiply_at
                if early:
                    messages(multiply_at[g], min(g + ADD_LAG, last_step))
                apply_silu(hs[tile], pre, c, all_cols)
            else:
                msg = msg_banks.tile([P, ROW_BLOCKS, M], F32, tag="msg")
                multiply_w2(msg, *codes[tile - 1], 0, ROW_BLOCKS)
                add_terms(pre, accs, terms[shift], c, halves_of_cols[0])
                apply_silu(hs[tile], pre, c, halves_of_cols[0])
                add_terms(pre, accs, terms[shift], c, halves_of_cols[1])
                apply_silu(hs[tile], pre, c, halves_of_cols[1])
                result = work.tile([P, ROW_BLOCKS, M], F32, bufs=4)
                nc.vector.tensor_tensor(out=result[:], in0=msg[:], in1=be2_all[:], op=ALU.add)
                finish_messages(g)
                store(result, *steps[g - F_PASSES][0:2], nc.gpsimd)
            if g in zero_at:
                if zero_at[g] < F_BLOCKS:
                    add_bias(zero_at[g])
                else:
                    apply_silu(zero_h, zero_pre, zero_at[g] - F_BLOCKS, all_cols)
            if g in quantise_at:
                tile = quantise_at[g]
                quantise_h(hs[tile], *codes[tile], 0, F_PASSES, all_cols)
                if g in held:
                    nc.gpsimd.memset(hs[tile][:, 0, 0, :], 0.0)
                    if coming:
                        k = (g - first_pair_step) % 8
                        if k == 0:
                            start_terms(coming)
                        for j in GPSIMD_TERMS[k] if g >= 38 else (k, k + 1):
                            distance_term(coming, j, False)
                    finish_messages(g)
            if g in multiply_at and not early:
                messages(multiply_at[g], min(g + ADD_LAG, last_step))
            if g == zero_quantise:
                quantise_h(zero_h, *codes[ZERO], 0, F_PASSES, all_cols)
            if g == zero_quantise + 2:
                messages(ZERO, g + ADD_LAG)

        quantise_h(hs[last_tile], *codes[last_tile], 0, 1, all_cols)
        result = work.tile([P, ROW_BLOCKS, M], F32, bufs=4)
        last_msgs = []
        for half, cols in enumerate(halves_of_cols):
            q0 = half * ROW_BLOCKS // 2
            q1 = q0 + ROW_BLOCKS // 2
            quantise_h(hs[last_tile], *codes[last_tile], 1, 2, cols)
            msg = banks.tile([P, ROW_BLOCKS // 2, M], F32, tag="bank")
            multiply_w2(msg, *codes[last_tile], q0, q1)
            last_msgs.append((msg, q0, q1))
        for msg, q0, q1 in last_msgs:
            nc.vector.tensor_tensor(out=result[:, q0:q1, :], in0=msg[:], in1=be2_all[:, q0:q1, :], op=ALU.add)
        store(result, *steps[last_step][0:2], nc.gpsimd)
